import numpy as np
import ml_dtypes


def mxq(x, axis, fmt="e4m3"):
    dtype, down = {"e4m3": (ml_dtypes.float8_e4m3fn, 7), "e5m2": (ml_dtypes.float8_e5m2, 14)}[fmt]
    v = np.moveaxis(np.asarray(x, np.float32).astype(ml_dtypes.bfloat16).astype(np.float64), axis, -1)
    blocks = v.reshape(v.shape[:-1] + (-1, 32))
    amax = np.abs(blocks).max(-1, keepdims=True)
    byte = np.maximum(np.where(amax > 0, np.frexp(amax)[1] - 1 + 127, 0) - down, 1)
    scale = np.exp2(byte - 127.0)
    codes = (blocks / scale).astype(np.float32).astype(dtype).astype(np.float64)
    return np.moveaxis((codes * scale).reshape(v.shape), -1, axis)


BF16 = ml_dtypes.bfloat16


def bf(x):
    return np.asarray(x, np.float32).astype(BF16)


def f64(x):
    return np.asarray(x).astype(np.float64)


N, M, D, R = 8192, 512, 512, 4


def softplus(x):
    return np.logaddexp(x, 0.0)


def setup_inputs():
    basis = np.random.standard_normal((R, D)) / np.sqrt(D)
    X = 0.5 * np.random.standard_normal((N, R)) @ basis + 0.5 * np.random.standard_normal((N, D)) / np.sqrt(D)
    X2 = 0.5 * np.random.standard_normal((M, R)) @ basis + 0.5 * np.random.standard_normal((M, D)) / np.sqrt(D)
    raw1 = np.log(np.expm1(1.0))
    return {"X": bf(X), "X2": bf(X2),
            "lengthscale": bf(raw1 + 0.3 * np.random.standard_normal((1, D))),
            "variance": bf(1.5 + 0.3 * np.random.standard_normal(1))}


def reference(X, X2, lengthscale, variance):
    l = softplus(f64(lengthscale))
    v = softplus(f64(variance))
    Xl = f64(X) / l
    X2l = f64(X2) / l
    xn = np.sum(Xl * Xl, axis=1)
    yn = np.sum(X2l * X2l, axis=1)
    cross = mxq(Xl, 1, "e4m3") @ mxq(X2l, 1, "e4m3").T
    d2 = np.maximum(xn[:, None] + yn[None, :] - 2.0 * cross, 0.0)
    return v[0] * np.exp(-0.5 * d2)

@@ -1,0 +1,186 @@
+import math
+from contextlib import ExitStack
+
+import concourse.mybir as mybir
+from concourse.masks import make_identity
+
+F32 = mybir.dt.float32
+BF16 = mybir.dt.bfloat16
+U32 = mybir.dt.uint32
+U8 = mybir.dt.uint8
+FP8X4 = mybir.dt.float8_e4m3fn_x4
+ACT = mybir.ActivationFunctionType
+ALU = mybir.AluOpType
+
+P = 128
+N_ROWS, M_ROWS, D_FEAT = 8192, 512, 512
+PACK = 4
+TILES = 4
+GROUP = P * TILES
+N_GROUPS = N_ROWS // GROUP
+FLOPS = 2 * N_ROWS * M_ROWS * D_FEAT
+SQRT_HALF = math.sqrt(0.5)
+
+GPSIMD_SCALE_GROUPS = (2, 5, 8, 11, 14)
+SCALAR_COPY_TILES = (1,)
+
+
+def tile_rbf_t_kernel(tc, X, X2, lengthscale, variance, out):
+    nc = tc.nc
+    x_view = X.rearrange("(g p j) k -> g p (j k)", p=P, j=TILES)
+    out_view = out.rearrange("(g p j) m -> g p (j m)", p=P, j=TILES)
+
+    with ExitStack() as stack:
+        const = stack.enter_context(tc.tile_pool(name="const", bufs=1))
+        xin = stack.enter_context(tc.tile_pool(name="xin", bufs=N_GROUPS))
+        work = stack.enter_context(tc.tile_pool(name="work", bufs=3))
+        outp = stack.enter_context(tc.tile_pool(name="outp", bufs=4))
+        psum_t = stack.enter_context(tc.psum_pool(name="psum_t", bufs=4))
+        psum_c = stack.enter_context(tc.psum_pool(name="psum_c", bufs=4))
+
+        raw = const.tile([P, 32], BF16, name="raw")
+        one_col = const.tile([P, 1], F32, name="one_col")
+        warm = const.tile([P, 1], F32, name="warm")
+        nc.vector.memset(raw[:], 0.0)
+        nc.vector.memset(one_col[:], 1.0)
+        nc.sync.dma_start(out=raw[:, 0:PACK], in_=lengthscale.rearrange("o (p t) -> p (o t)", t=PACK))
+        nc.sync.dma_start(out=raw[:, 16:17], in_=variance.partition_broadcast(P))
+        nc.scalar.activation(out=warm[:], in_=one_col[:], func=ACT.Exp)
+
+        x2g = const.tile([P, TILES, D_FEAT], BF16, name="x2g")
+        nc.sync.dma_start(out=x2g[:], in_=X2.rearrange("(j p) k -> p j k", p=P))
+        xgs = []
+        for g in range(N_GROUPS):
+            xg = xin.tile([P, TILES * D_FEAT], BF16, name="xg")
+            nc.sync.dma_start(out=xg[:], in_=x_view[g])
+            xgs.append(xg)
+
+        ident = const.tile([P, P], F32, name="ident")
+        make_identity(nc, ident[:])
+
+        W = 17
+        absx = const.tile([P, W], F32, name="absx")
+        expx = const.tile([P, W], F32, name="expx")
+        logx = const.tile([P, W], F32, name="logx")
+        soft = const.tile([P, W], F32, name="soft")
+        invl4 = const.tile([P, PACK], F32, name="invl4")
+        lnv = const.tile([P, 1], F32, name="lnv")
+        nc.scalar.activation(out=absx[:], in_=raw[:, 0:W], func=ACT.Abs)
+        nc.scalar.activation(out=expx[:], in_=absx[:], func=ACT.Exp, scale=-1.0)
+        nc.scalar.activation(out=logx[:], in_=expx[:], func=ACT.Ln, bias=one_col[:, 0:1])
+        nc.vector.scalar_tensor_tensor(
+            out=soft[:], in0=raw[:, 0:W], scalar=0.0, in1=logx[:], op0=ALU.max, op1=ALU.add
+        )
+        nc.vector.reciprocal(out=invl4[:], in_=soft[:, 0:PACK])
+        nc.scalar.activation(out=lnv[:], in_=soft[:, 16:17], func=ACT.Ln)
+        v_col = soft[:, 16:17]
+
+        invl_ps = psum_t.tile([P, PACK, P], F32, name="tb")
+        for t in range(PACK):
+            nc.tensor.matmul(
+                out=invl_ps[:, t, :],
+                lhsT=invl4[:, t : t + 1].to_broadcast([P, P]),
+                rhs=ident[:],
+                start=True,
+                stop=True,
+            )
+        invl_b = const.tile([P, D_FEAT], F32, name="invl_b")
+        nc.vector.tensor_copy(
+            out=invl_b[:].rearrange("p (j t) -> p j t", t=PACK),
+            in_=invl_ps[:].rearrange("p t j -> p j t"),
+        )
+        invl_rep = invl_b[:].unsqueeze(1).to_broadcast([P, TILES, D_FEAT])
+
+        half_xn = const.tile([P, N_GROUPS * TILES], F32, name="half_xn")
+        half_yn = const.tile([P, TILES], F32, name="half_yn")
+
+        def front(src, norms, first_col, codes, scales, scale_engine):
+            xl = work.tile([P, TILES, D_FEAT], F32, name="xl")
+            scale_engine.tensor_tensor(
+                out=xl[:], in0=src.rearrange("p (j k) -> p j k", j=TILES), in1=invl_rep, op=ALU.mult
+            )
+            grouped = work.tile([P, TILES, P, PACK], BF16, name="grouped", align_bytes=64)
+            for j in range(TILES):
+                junk = work.tile([P, D_FEAT], BF16, name="junk")
+                nc.scalar.activation(
+                    out=junk[:],
+                    in_=xl[:, j, :],
+                    func=ACT.Square,
+                    scale=SQRT_HALF,
+                    accum_out=norms[:, first_col + j : first_col + j + 1],
+                )
+                tb = psum_t.tile([P, PACK, P], F32, name="tb")
+                for t in range(PACK):
+                    nc.tensor.transpose(tb[:, t, :], xl[:, j, t * P : (t + 1) * P], ident[:])
+                if j in SCALAR_COPY_TILES:
+                    nc.scalar.copy(out=grouped[:, j, :, :], in_=tb[:].rearrange("p t r -> p r t"))
+                else:
+                    nc.vector.tensor_copy(out=grouped[:, j, :, :], in_=tb[:].rearrange("p t r -> p r t"))
+            nc.vector.quantize_mx(
+                out=codes.bitcast(FP8X4),
+                scales=scales,
+                in_=grouped[:].rearrange("p j r t -> p (j r t)"),
+            )
+
+        x2_codes = const.tile([P, M_ROWS], U32, name="x2_codes", align_bytes=64)
+        x2_scales = const.tile([P, M_ROWS], U8, name="x2_scales", align_bytes=64)
+        front(x2g[:].rearrange("p j k -> p (j k)"), half_yn, 0, x2_codes[:], x2_scales[:], nc.vector)
+        yn_ps = psum_t.tile([P, TILES, P], F32, name="tb")
+        for j in range(TILES):
+            nc.tensor.matmul(
+                out=yn_ps[:, j, :],
+                lhsT=half_yn[:, j : j + 1].to_broadcast([P, P]),
+                rhs=ident[:],
+                start=True,
+                stop=True,
+            )
+        col_term = const.tile([P, M_ROWS], F32, name="col_term")
+        nc.vector.tensor_scalar(
+            out=col_term[:],
+            in0=yn_ps[:].rearrange("p j r -> p (j r)"),
+            scalar1=-1.0,
+            scalar2=lnv[:, 0:1],
+            op0=ALU.mult,
+            op1=ALU.add,
+        )
+
+        quantised = {}
+
+        def back(g):
+            codes, scales = quantised[g]
+            res = outp.tile([P, TILES, M_ROWS], F32, name="res")
+            for j in range(TILES):
+                cols = slice(j * P, (j + 1) * P)
+                cross = psum_c.tile([P, M_ROWS], F32, name="cross")
+                nc.tensor.matmul_mx(
+                    out=cross[:],
+                    lhsT=codes[:, cols].bitcast(FP8X4),
+                    lhsT_scale=scales[:, cols],
+                    rhs=x2_codes[:].bitcast(FP8X4),
+                    rhs_scale=x2_scales[:],
+                    start=True,
+                    stop=True,
+                )
+                i = g * TILES + j
+                nc.vector.scalar_tensor_tensor(
+                    out=res[:, j, :],
+                    in0=cross[:],
+                    scalar=half_xn[:, i : i + 1],
+                    in1=col_term[:],
+                    op0=ALU.subtract,
+                    op1=ALU.add,
+                )
+            flat = res[:].rearrange("p j m -> p (j m)")
+            nc.scalar.activation(out=flat, in_=flat, func=ACT.Exp)
+            nc.gpsimd.tensor_scalar(out=flat, in0=flat, scalar1=v_col, scalar2=0.0, op0=ALU.min, op1=ALU.max)
+            nc.sync.dma_start(out=out_view[g], in_=flat)
+
+        for g in range(N_GROUPS + 1):
+            if g < N_GROUPS:
+                codes = work.tile([P, GROUP], U32, name="codes", align_bytes=64)
+                scales = work.tile([P, GROUP], U8, name="scales", align_bytes=64)
+                quantised[g] = (codes, scales)
+                engine = nc.gpsimd if g in GPSIMD_SCALE_GROUPS else nc.vector
+                front(xgs[g][:], half_xn, g * TILES, codes[:], scales[:], engine)
+            if g >= 1:
+                back(g - 1)

@@ -11,18 +11,25 @@ U8 = mybir.dt.uint8
 FP8X4 = mybir.dt.float8_e4m3fn_x4
 ACT = mybir.ActivationFunctionType
 ALU = mybir.AluOpType
+AXIS = mybir.AxisListType
 
 P = 128
 N_ROWS, M_ROWS, D_FEAT = 8192, 512, 512
 PACK = 4
 TILES = 4
+PAIR = 2
+UNIT = PAIR * P
 GROUP = P * TILES
-N_GROUPS = N_ROWS // GROUP
+N_GROUPS = N_ROWS // GROUP + 1
+N_UNITS = 2 * N_GROUPS
 FLOPS = 2 * N_ROWS * M_ROWS * D_FEAT
 SQRT_HALF = math.sqrt(0.5)
 
-GPSIMD_SCALE_GROUPS = (2, 5, 8, 11, 14)
-SCALAR_COPY_TILES = (1,)
+GPSIMD_CLAMP_GROUPS = tuple(range(1, 15))
+VECTOR_REDUCE_GROUPS = ()
+LAG_EXP_VECTOR = 1
+LAG_EXP_GPSIMD = 4
+LAG_F = 3
 
 
 def tile_rbf_t_kernel(tc, X, X2, lengthscale, variance, out):
@@ -31,39 +38,65 @@ def tile_rbf_t_kernel(tc, X, X2, lengthscale, variance, out):
     out_view = out.rearrange("(g p j) m -> g p (j m)", p=P, j=TILES)
 
     with ExitStack() as stack:
+        stack.enter_context(tc.manual_schedule())
         const = stack.enter_context(tc.tile_pool(name="const", bufs=1))
         xin = stack.enter_context(tc.tile_pool(name="xin", bufs=N_GROUPS))
         work = stack.enter_context(tc.tile_pool(name="work", bufs=3))
-        outp = stack.enter_context(tc.tile_pool(name="outp", bufs=4))
-        psum_t = stack.enter_context(tc.psum_pool(name="psum_t", bufs=4))
-        psum_c = stack.enter_context(tc.psum_pool(name="psum_c", bufs=4))
+        held = stack.enter_context(tc.tile_pool(name="held", bufs=LAG_F + 3))
+        small = stack.enter_context(tc.tile_pool(name="small", bufs=4))
+        outp = stack.enter_context(tc.tile_pool(name="outp", bufs=6))
+        psum_t = stack.enter_context(tc.psum_pool(name="psum_t", bufs=3))
+        psum_s = stack.enter_context(tc.psum_pool(name="psum_s", bufs=2))
+        psum_c = stack.enter_context(tc.psum_pool(name="psum_c", bufs=3))
 
         raw = const.tile([P, 32], BF16, name="raw")
         one_col = const.tile([P, 1], F32, name="one_col")
         warm = const.tile([P, 1], F32, name="warm")
         nc.vector.memset(raw[:], 0.0)
         nc.vector.memset(one_col[:], 1.0)
-        nc.sync.dma_start(out=raw[:, 0:PACK], in_=lengthscale.rearrange("o (p t) -> p (o t)", t=PACK))
+        nc.sync.dma_start(
+            out=raw[:, 0:PACK].rearrange("p (u e) -> p u e", e=2),
+            in_=lengthscale.rearrange("o (u p e) -> p (o u) e", p=P, e=2),
+        )
         nc.sync.dma_start(out=raw[:, 16:17], in_=variance.partition_broadcast(P))
         nc.scalar.activation(out=warm[:], in_=one_col[:], func=ACT.Exp)
-
-        x2g = const.tile([P, TILES, D_FEAT], BF16, name="x2g")
-        nc.sync.dma_start(out=x2g[:], in_=X2.rearrange("(j p) k -> p j k", p=P))
-        xgs = []
+        sources = []
         for g in range(N_GROUPS):
             xg = xin.tile([P, TILES * D_FEAT], BF16, name="xg")
-            nc.sync.dma_start(out=xg[:], in_=x_view[g])
-            xgs.append(xg)
+            if g == 0:
+                nc.sync.dma_start(
+                    out=xg[:].rearrange("p (j k) -> p j k", j=TILES), in_=X2.rearrange("(j p) k -> p j k", p=P)
+                )
+            else:
+                nc.sync.dma_start(out=xg[:], in_=x_view[g - 1])
+            sources.append(xg[:].bitcast(F32).rearrange("p (j w) -> p j w", j=TILES))
 
         ident = const.tile([P, P], F32, name="ident")
         make_identity(nc, ident[:])
+
+        banks, squares, operands, sums, norms, results = {}, {}, {}, {}, {}, {}
+
+        def transpose_unit(b):
+            tb = psum_t.tile([P, 2 * UNIT], F32, name="tb")
+            banks[b] = tb[:].bitcast(BF16)
+            for u in range(2):
+                for h in range(PAIR):
+                    nc.tensor.transpose(
+                        tb[:, (u * PAIR + h) * P : (u * PAIR + h + 1) * P],
+                        sources[b // 2][:, (b % 2) * PAIR + h, u * P : (u + 1) * P],
+                        ident[:],
+                    )
+
+        transpose_unit(0)
+        transpose_unit(1)
 
         W = 17
         absx = const.tile([P, W], F32, name="absx")
         expx = const.tile([P, W], F32, name="expx")
         logx = const.tile([P, W], F32, name="logx")
         soft = const.tile([P, W], F32, name="soft")
-        invl4 = const.tile([P, PACK], F32, name="invl4")
+        invl = const.tile([P, PACK], F32, name="invl")
+        sinv = const.tile([P, PACK], F32, name="sinv")
         lnv = const.tile([P, 1], F32, name="lnv")
         nc.scalar.activation(out=absx[:], in_=raw[:, 0:W], func=ACT.Abs)
         nc.scalar.activation(out=expx[:], in_=absx[:], func=ACT.Exp, scale=-1.0)
@@ -71,116 +104,173 @@ def tile_rbf_t_kernel(tc, X, X2, lengthscale, variance, out):
         nc.vector.scalar_tensor_tensor(
             out=soft[:], in0=raw[:, 0:W], scalar=0.0, in1=logx[:], op0=ALU.max, op1=ALU.add
         )
-        nc.vector.reciprocal(out=invl4[:], in_=soft[:, 0:PACK])
+        nc.vector.reciprocal(out=invl[:], in_=soft[:, 0:PACK])
+        nc.vector.tensor_scalar(out=sinv[:], in0=invl[:], scalar1=SQRT_HALF, scalar2=None, op0=ALU.mult)
         nc.scalar.activation(out=lnv[:], in_=soft[:, 16:17], func=ACT.Ln)
-        v_col = soft[:, 16:17]
-
-        invl_ps = psum_t.tile([P, PACK, P], F32, name="tb")
-        for t in range(PACK):
-            nc.tensor.matmul(
-                out=invl_ps[:, t, :],
-                lhsT=invl4[:, t : t + 1].to_broadcast([P, P]),
-                rhs=ident[:],
-                start=True,
-                stop=True,
-            )
-        invl_b = const.tile([P, D_FEAT], F32, name="invl_b")
-        nc.vector.tensor_copy(
-            out=invl_b[:].rearrange("p (j t) -> p j t", t=PACK),
-            in_=invl_ps[:].rearrange("p t j -> p j t"),
-        )
-        invl_rep = invl_b[:].unsqueeze(1).to_broadcast([P, TILES, D_FEAT])
-
-        half_xn = const.tile([P, N_GROUPS * TILES], F32, name="half_xn")
-        half_yn = const.tile([P, TILES], F32, name="half_yn")
-
-        def front(src, norms, first_col, codes, scales, scale_engine):
-            xl = work.tile([P, TILES, D_FEAT], F32, name="xl")
-            scale_engine.tensor_tensor(
-                out=xl[:], in0=src.rearrange("p (j k) -> p j k", j=TILES), in1=invl_rep, op=ALU.mult
-            )
-            grouped = work.tile([P, TILES, P, PACK], BF16, name="grouped", align_bytes=64)
-            for j in range(TILES):
-                junk = work.tile([P, D_FEAT], BF16, name="junk")
-                nc.scalar.activation(
-                    out=junk[:],
-                    in_=xl[:, j, :],
-                    func=ACT.Square,
-                    scale=SQRT_HALF,
-                    accum_out=norms[:, first_col + j : first_col + j + 1],
-                )
-                tb = psum_t.tile([P, PACK, P], F32, name="tb")
-                for t in range(PACK):
-                    nc.tensor.transpose(tb[:, t, :], xl[:, j, t * P : (t + 1) * P], ident[:])
-                if j in SCALAR_COPY_TILES:
-                    nc.scalar.copy(out=grouped[:, j, :, :], in_=tb[:].rearrange("p t r -> p r t"))
-                else:
-                    nc.vector.tensor_copy(out=grouped[:, j, :, :], in_=tb[:].rearrange("p t r -> p r t"))
-            nc.vector.quantize_mx(
-                out=codes.bitcast(FP8X4),
-                scales=scales,
-                in_=grouped[:].rearrange("p j r t -> p (j r t)"),
-            )
+        invl_rep = invl[:].unsqueeze(1).to_broadcast([P, UNIT, PACK])
 
         x2_codes = const.tile([P, M_ROWS], U32, name="x2_codes", align_bytes=64)
         x2_scales = const.tile([P, M_ROWS], U8, name="x2_scales", align_bytes=64)
-        front(x2g[:].rearrange("p j k -> p (j k)"), half_yn, 0, x2_codes[:], x2_scales[:], nc.vector)
-        yn_ps = psum_t.tile([P, TILES, P], F32, name="tb")
-        for j in range(TILES):
-            nc.tensor.matmul(
-                out=yn_ps[:, j, :],
-                lhsT=half_yn[:, j : j + 1].to_broadcast([P, P]),
-                rhs=ident[:],
-                start=True,
-                stop=True,
-            )
         col_term = const.tile([P, M_ROWS], F32, name="col_term")
-        nc.vector.tensor_scalar(
-            out=col_term[:],
-            in0=yn_ps[:].rearrange("p j r -> p (j r)"),
-            scalar1=-1.0,
-            scalar2=lnv[:, 0:1],
-            op0=ALU.mult,
-            op1=ALU.add,
-        )
 
-        quantised = {}
+        def scale_unit(b):
+            grouped = work.tile([P, UNIT, PACK], BF16, name="grouped", align_bytes=64)
+            nc.vector.tensor_tensor(
+                out=grouped[:].rearrange("p r (u e) -> p r u e", e=2),
+                in0=banks[b].rearrange("p (u r e) -> p r u e", u=2, e=2),
+                in1=invl_rep.rearrange("p r (u e) -> p r u e", e=2),
+                op=ALU.mult,
+            )
+            return grouped
 
-        def back(g):
-            codes, scales = quantised[g]
-            res = outp.tile([P, TILES, M_ROWS], F32, name="res")
+        def square_unit(b):
+            planes = banks[b].rearrange("p (u r e) -> p u e r", u=2, e=2)
+            sq = work.tile([P, PACK, UNIT], F32, name="sq")
+            squares[b] = sq
+            for u in range(2):
+                for e in range(2):
+                    t = 2 * u + e
+                    nc.scalar.activation(
+                        out=sq[:, t, :], in_=planes[:, u, e, :], func=ACT.Square, scale=sinv[:, t : t + 1]
+                    )
+
+        def quantise_unit(b, grouped):
+            if b < 2:
+                cols = slice(b * UNIT, (b + 1) * UNIT)
+                codes, scales = x2_codes[:, cols], x2_scales[:, cols]
+            else:
+                codes_t = held.tile([P, UNIT], U32, name="codes", align_bytes=64)
+                scales_t = held.tile([P, UNIT], U8, name="scales", align_bytes=64)
+                codes, scales = codes_t[:], scales_t[:]
+            operands[b] = (codes, scales)
+            nc.vector.quantize_mx(
+                out=codes.bitcast(FP8X4), scales=scales, in_=grouped[:].rearrange("p r t -> p (r t)")
+            )
+
+        def sum_unit(b):
+            g = b // 2
+            if b % 2 == 0:
+                sums_t = psum_s.tile([P, TILES, P], F32, name="sums")
+                sums[g] = sums_t
+            for h in range(PAIR):
+                for t in range(PACK):
+                    nc.tensor.matmul(
+                        out=sums[g][:, (b % 2) * PAIR + h, :],
+                        lhsT=squares[b][:, t, h * P : (h + 1) * P],
+                        rhs=ident[:],
+                        is_transpose=True,
+                        start=(t == 0),
+                        stop=(t == PACK - 1),
+                    )
+
+        def reduce_group(g):
+            norm = small.tile([P, TILES], F32, name="norm")
+            norms[g] = norm
+            if g in VECTOR_REDUCE_GROUPS:
+                nc.vector.tensor_reduce(out=norm[:], in_=sums[g][:], axis=AXIS.X, op=ALU.add)
+            else:
+                for j in range(TILES):
+                    junk = work.tile([P, P], BF16, name="junk")
+                    nc.scalar.activation(
+                        out=junk[:], in_=sums[g][:, j, :], func=ACT.Copy, accum_out=norm[:, j : j + 1]
+                    )
+
+        def spread_column_norms():
+            yn_ps = psum_s.tile([P, TILES, P], F32, name="sums")
             for j in range(TILES):
-                cols = slice(j * P, (j + 1) * P)
-                cross = psum_c.tile([P, M_ROWS], F32, name="cross")
-                nc.tensor.matmul_mx(
-                    out=cross[:],
-                    lhsT=codes[:, cols].bitcast(FP8X4),
-                    lhsT_scale=scales[:, cols],
-                    rhs=x2_codes[:].bitcast(FP8X4),
-                    rhs_scale=x2_scales[:],
+                nc.tensor.matmul(
+                    out=yn_ps[:, j, :],
+                    lhsT=norms[0][:, j : j + 1].to_broadcast([P, P]),
+                    rhs=ident[:],
                     start=True,
                     stop=True,
                 )
-                i = g * TILES + j
-                nc.vector.scalar_tensor_tensor(
-                    out=res[:, j, :],
-                    in0=cross[:],
-                    scalar=half_xn[:, i : i + 1],
-                    in1=col_term[:],
-                    op0=ALU.subtract,
-                    op1=ALU.add,
-                )
-            flat = res[:].rearrange("p j m -> p (j m)")
-            nc.scalar.activation(out=flat, in_=flat, func=ACT.Exp)
-            nc.gpsimd.tensor_scalar(out=flat, in0=flat, scalar1=v_col, scalar2=0.0, op0=ALU.min, op1=ALU.max)
-            nc.sync.dma_start(out=out_view[g], in_=flat)
+            return yn_ps
 
-        for g in range(N_GROUPS + 1):
-            if g < N_GROUPS:
-                codes = work.tile([P, GROUP], U32, name="codes", align_bytes=64)
-                scales = work.tile([P, GROUP], U8, name="scales", align_bytes=64)
-                quantised[g] = (codes, scales)
-                engine = nc.gpsimd if g in GPSIMD_SCALE_GROUPS else nc.vector
-                front(xgs[g][:], half_xn, g * TILES, codes[:], scales[:], engine)
-            if g >= 1:
-                back(g - 1)
+        def negate_column_norms(yn_ps):
+            nc.vector.tensor_scalar(
+                out=col_term[:],
+                in0=yn_ps[:].rearrange("p j r -> p (j r)"),
+                scalar1=-1.0,
+                scalar2=None,
+                op0=ALU.mult,
+            )
+
+        def multiply_tile(b, h):
+            codes, scales = operands[b]
+            cols = slice(h * P, (h + 1) * P)
+            cross = psum_c.tile([P, M_ROWS], F32, name="cross")
+            nc.tensor.matmul_mx(
+                out=cross[:],
+                lhsT=codes[:, cols].bitcast(FP8X4),
+                lhsT_scale=scales[:, cols],
+                rhs=x2_codes[:].bitcast(FP8X4),
+                rhs_scale=x2_scales[:],
+                start=True,
+                stop=True,
+            )
+            return cross
+
+        def exponent_tile(b, h, cross):
+            g = b // 2
+            j = (b % 2) * PAIR + h
+            if j == 0:
+                res = outp.tile([P, TILES, M_ROWS], F32, name="res")
+                results[g] = res
+            nc.vector.scalar_tensor_tensor(
+                out=results[g][:, j, :],
+                in0=cross[:],
+                scalar=norms[g][:, j : j + 1],
+                in1=col_term[:],
+                op0=ALU.subtract,
+                op1=ALU.add,
+            )
+
+        def clamp_group(g):
+            flat = results[g][:].rearrange("p j m -> p (j m)")
+            if g in GPSIMD_CLAMP_GROUPS:
+                nc.gpsimd.tensor_scalar(
+                    out=flat, in0=flat, scalar1=0.0, scalar2=-1.0e30, op0=ALU.min, op1=ALU.max
+                )
+            else:
+                nc.vector.tensor_scalar(out=flat, in0=flat, scalar1=0.0, scalar2=None, op0=ALU.min)
+
+        def finish_group(g):
+            flat = results[g][:].rearrange("p j m -> p (j m)")
+            nc.scalar.activation(out=flat, in_=flat, func=ACT.Exp, bias=lnv[:, 0:1])
+            nc.sync.dma_start(out=out_view[g - 1], in_=flat)
+
+        square_unit(0)
+        waiting = []
+        yn_box = []
+        for s in range(N_UNITS + LAG_F + max(LAG_EXP_VECTOR, LAG_EXP_GPSIMD) + 1):
+            b = s - LAG_F
+            live = 2 <= b < N_UNITS
+            crosses = [multiply_tile(b, h) for h in range(PAIR)] if live else []
+            if s + 2 < N_UNITS:
+                transpose_unit(s + 2)
+            if s == 2:
+                yn_box.append(spread_column_norms())
+            if s + 1 < N_UNITS:
+                square_unit(s + 1)
+            grouped = scale_unit(s) if s < N_UNITS else None
+            if s == 3:
+                negate_column_norms(yn_box[0])
+            if s < N_UNITS:
+                sum_unit(s)
+                if s % 2 == 1:
+                    reduce_group(s // 2)
+            if live:
+                exponent_tile(b, 0, crosses[0])
+            if s < N_UNITS:
+                quantise_unit(s, grouped)
+            if live:
+                exponent_tile(b, 1, crosses[1])
+                if b % 2 == 1:
+                    g = b // 2
+                    clamp_group(g)
+                    waiting.append((s + (LAG_EXP_GPSIMD if g in GPSIMD_CLAMP_GROUPS else LAG_EXP_VECTOR), g))
+            for due, g in sorted(waiting):
+                if due <= s:
+                    finish_group(g)
+            waiting = [entry for entry in waiting if entry[0] > s]

@@ -25,8 +25,9 @@ N_UNITS = 2 * N_GROUPS
 FLOPS = 2 * N_ROWS * M_ROWS * D_FEAT
 SQRT_HALF = math.sqrt(0.5)
 
-GPSIMD_CLAMP_GROUPS = tuple(range(1, 15))
+GPSIMD_CLAMP_GROUPS = (1, 2, 3, 5, 6, 7, 9, 10, 11, 13, 14)
 VECTOR_REDUCE_GROUPS = ()
+FINE_GROUPS = (16,)
 LAG_EXP_VECTOR = 1
 LAG_EXP_GPSIMD = 4
 LAG_F = 3
@@ -226,8 +227,8 @@ def tile_rbf_t_kernel(tc, X, X2, lengthscale, variance, out):
                 op1=ALU.add,
             )
 
-        def clamp_group(g):
-            flat = results[g][:].rearrange("p j m -> p (j m)")
+        def clamp_tiles(g, first, count):
+            flat = results[g][:, first : first + count, :].rearrange("p j m -> p (j m)")
             if g in GPSIMD_CLAMP_GROUPS:
                 nc.gpsimd.tensor_scalar(
                     out=flat, in0=flat, scalar1=0.0, scalar2=-1.0e30, op0=ALU.min, op1=ALU.max
@@ -235,10 +236,10 @@ def tile_rbf_t_kernel(tc, X, X2, lengthscale, variance, out):
             else:
                 nc.vector.tensor_scalar(out=flat, in0=flat, scalar1=0.0, scalar2=None, op0=ALU.min)
 
-        def finish_group(g):
-            flat = results[g][:].rearrange("p j m -> p (j m)")
+        def finish_tiles(g, first, count):
+            flat = results[g][:, first : first + count, :].rearrange("p j m -> p (j m)")
             nc.scalar.activation(out=flat, in_=flat, func=ACT.Exp, bias=lnv[:, 0:1])
-            nc.sync.dma_start(out=out_view[g - 1], in_=flat)
+            nc.sync.dma_start(out=out_view[g - 1][:, first * M_ROWS : (first + count) * M_ROWS], in_=flat)
 
         square_unit(0)
         waiting = []
@@ -266,11 +267,14 @@ def tile_rbf_t_kernel(tc, X, X2, lengthscale, variance, out):
                 quantise_unit(s, grouped)
             if live:
                 exponent_tile(b, 1, crosses[1])
-                if b % 2 == 1:
-                    g = b // 2
-                    clamp_group(g)
-                    waiting.append((s + (LAG_EXP_GPSIMD if g in GPSIMD_CLAMP_GROUPS else LAG_EXP_VECTOR), g))
-            for due, g in sorted(waiting):
+                g = b // 2
+                if g in FINE_GROUPS:
+                    clamp_tiles(g, (b % 2) * PAIR, PAIR)
+                    waiting.append((s, g, (b % 2) * PAIR, PAIR))
+                elif b % 2 == 1:
+                    clamp_tiles(g, 0, TILES)
+                    waiting.append((s + (LAG_EXP_GPSIMD if g in GPSIMD_CLAMP_GROUPS else LAG_EXP_VECTOR), g, 0, TILES))
+            for due, g, first, count in sorted(waiting):
                 if due <= s:
-                    finish_group(g)
+                    finish_tiles(g, first, count)
             waiting = [entry for entry in waiting if entry[0] > s]

@@ -30,6 +30,7 @@ VECTOR_REDUCE_GROUPS = ()
 FINE_GROUPS = (16,)
 LAG_EXP_VECTOR = 1
 LAG_EXP_GPSIMD = 4
+MX_REPEAT = 2
 LAG_F = 3
 
 
@@ -201,15 +202,16 @@ def tile_rbf_t_kernel(tc, X, X2, lengthscale, variance, out):
             codes, scales = operands[b]
             cols = slice(h * P, (h + 1) * P)
             cross = psum_c.tile([P, M_ROWS], F32, name="cross")
-            nc.tensor.matmul_mx(
-                out=cross[:],
-                lhsT=codes[:, cols].bitcast(FP8X4),
-                lhsT_scale=scales[:, cols],
-                rhs=x2_codes[:].bitcast(FP8X4),
-                rhs_scale=x2_scales[:],
-                start=True,
-                stop=True,
-            )
+            for rep in range(MX_REPEAT):
+                nc.tensor.matmul_mx(
+                    out=cross[:],
+                    lhsT=codes[:, cols].bitcast(FP8X4),
+                    lhsT_scale=scales[:, cols],
+                    rhs=x2_codes[:].bitcast(FP8X4),
+                    rhs_scale=x2_scales[:],
+                    start=True,
+                    stop=True,
+                )
             return cross
 
         def exponent_tile(b, h, cross):

@@ -25,12 +25,11 @@ N_UNITS = 2 * N_GROUPS
 FLOPS = 2 * N_ROWS * M_ROWS * D_FEAT
 SQRT_HALF = math.sqrt(0.5)
 
-GPSIMD_CLAMP_GROUPS = (1, 2, 3, 5, 6, 7, 9, 10, 11, 13, 14)
+GPSIMD_CLAMP_GROUPS = tuple(range(1, 14))
 VECTOR_REDUCE_GROUPS = ()
-FINE_GROUPS = (16,)
+FINE_GROUPS = (15, 16)
 LAG_EXP_VECTOR = 1
 LAG_EXP_GPSIMD = 4
-MX_REPEAT = 2
 LAG_F = 3
 
 
@@ -171,7 +170,7 @@ def tile_rbf_t_kernel(tc, X, X2, lengthscale, variance, out):
             if g in VECTOR_REDUCE_GROUPS:
                 nc.vector.tensor_reduce(out=norm[:], in_=sums[g][:], axis=AXIS.X, op=ALU.add)
             else:
-                for j in range(TILES):
+                for j in reversed(range(TILES)):
                     junk = work.tile([P, P], BF16, name="junk")
                     nc.scalar.activation(
                         out=junk[:], in_=sums[g][:, j, :], func=ACT.Copy, accum_out=norm[:, j : j + 1]
@@ -202,22 +201,21 @@ def tile_rbf_t_kernel(tc, X, X2, lengthscale, variance, out):
             codes, scales = operands[b]
             cols = slice(h * P, (h + 1) * P)
             cross = psum_c.tile([P, M_ROWS], F32, name="cross")
-            for rep in range(MX_REPEAT):
-                nc.tensor.matmul_mx(
-                    out=cross[:],
-                    lhsT=codes[:, cols].bitcast(FP8X4),
-                    lhsT_scale=scales[:, cols],
-                    rhs=x2_codes[:].bitcast(FP8X4),
-                    rhs_scale=x2_scales[:],
-                    start=True,
-                    stop=True,
-                )
+            nc.tensor.matmul_mx(
+                out=cross[:],
+                lhsT=codes[:, cols].bitcast(FP8X4),
+                lhsT_scale=scales[:, cols],
+                rhs=x2_codes[:].bitcast(FP8X4),
+                rhs_scale=x2_scales[:],
+                start=True,
+                stop=True,
+            )
             return cross
 
         def exponent_tile(b, h, cross):
             g = b // 2
             j = (b % 2) * PAIR + h
-            if j == 0:
+            if g not in results:
                 res = outp.tile([P, TILES, M_ROWS], F32, name="res")
                 results[g] = res
             nc.vector.scalar_tensor_tensor(
@@ -252,23 +250,23 @@ def tile_rbf_t_kernel(tc, X, X2, lengthscale, variance, out):
             crosses = [multiply_tile(b, h) for h in range(PAIR)] if live else []
             if s + 2 < N_UNITS:
                 transpose_unit(s + 2)
-            if s == 2:
+            if s == 3:
                 yn_box.append(spread_column_norms())
             if s + 1 < N_UNITS:
                 square_unit(s + 1)
             grouped = scale_unit(s) if s < N_UNITS else None
-            if s == 3:
+            if s == 4:
                 negate_column_norms(yn_box[0])
             if s < N_UNITS:
                 sum_unit(s)
-                if s % 2 == 1:
-                    reduce_group(s // 2)
+            if s % 2 == 0 and 0 <= (s - 2) // 2 < N_GROUPS and s >= 2:
+                reduce_group((s - 2) // 2)
             if live:
-                exponent_tile(b, 0, crosses[0])
+                exponent_tile(b, 1, crosses[1])
             if s < N_UNITS:
                 quantise_unit(s, grouped)
             if live:
-                exponent_tile(b, 1, crosses[1])
+                exponent_tile(b, 0, crosses[0])
                 g = b // 2
                 if g in FINE_GROUPS:
                     clamp_tiles(g, (b % 2) * PAIR, PAIR)

@@ -11,7 +11,6 @@ U8 = mybir.dt.uint8
 FP8X4 = mybir.dt.float8_e4m3fn_x4
 ACT = mybir.ActivationFunctionType
 ALU = mybir.AluOpType
-AXIS = mybir.AxisListType
 
 P = 128
 N_ROWS, M_ROWS, D_FEAT = 8192, 512, 512
@@ -25,11 +24,9 @@ N_UNITS = 2 * N_GROUPS
 FLOPS = 2 * N_ROWS * M_ROWS * D_FEAT
 SQRT_HALF = math.sqrt(0.5)
 
-GPSIMD_CLAMP_GROUPS = tuple(range(1, 14))
-VECTOR_REDUCE_GROUPS = ()
+GPSIMD_CLAMP_GROUPS = tuple(range(1, 16))
 FINE_GROUPS = (15, 16)
-LAG_EXP_VECTOR = 1
-LAG_EXP_GPSIMD = 4
+LAG_EXP = 1
 LAG_F = 3
 
 
@@ -167,14 +164,9 @@ def tile_rbf_t_kernel(tc, X, X2, lengthscale, variance, out):
         def reduce_group(g):
             norm = small.tile([P, TILES], F32, name="norm")
             norms[g] = norm
-            if g in VECTOR_REDUCE_GROUPS:
-                nc.vector.tensor_reduce(out=norm[:], in_=sums[g][:], axis=AXIS.X, op=ALU.add)
-            else:
-                for j in reversed(range(TILES)):
-                    junk = work.tile([P, P], BF16, name="junk")
-                    nc.scalar.activation(
-                        out=junk[:], in_=sums[g][:, j, :], func=ACT.Copy, accum_out=norm[:, j : j + 1]
-                    )
+            for j in reversed(range(TILES)):
+                junk = work.tile([P, P], BF16, name="junk")
+                nc.scalar.activation(out=junk[:], in_=sums[g][:, j, :], func=ACT.Copy, accum_out=norm[:, j : j + 1])
 
         def spread_column_norms():
             yn_ps = psum_s.tile([P, TILES, P], F32, name="sums")
@@ -226,14 +218,15 @@ def tile_rbf_t_kernel(tc, X, X2, lengthscale, variance, out):
                 op0=ALU.subtract,
                 op1=ALU.add,
             )
+            if g in GPSIMD_CLAMP_GROUPS:
+                nc.gpsimd.tensor_scalar(
+                    out=results[g][:, j, :], in0=results[g][:, j, :],
+                    scalar1=0.0, scalar2=-1.0e30, op0=ALU.min, op1=ALU.max,
+                )
 
         def clamp_tiles(g, first, count):
             flat = results[g][:, first : first + count, :].rearrange("p j m -> p (j m)")
-            if g in GPSIMD_CLAMP_GROUPS:
-                nc.gpsimd.tensor_scalar(
-                    out=flat, in0=flat, scalar1=0.0, scalar2=-1.0e30, op0=ALU.min, op1=ALU.max
-                )
-            else:
+            if g not in GPSIMD_CLAMP_GROUPS:
                 nc.vector.tensor_scalar(out=flat, in0=flat, scalar1=0.0, scalar2=None, op0=ALU.min)
 
         def finish_tiles(g, first, count):
@@ -244,7 +237,7 @@ def tile_rbf_t_kernel(tc, X, X2, lengthscale, variance, out):
         square_unit(0)
         waiting = []
         yn_box = []
-        for s in range(N_UNITS + LAG_F + max(LAG_EXP_VECTOR, LAG_EXP_GPSIMD) + 1):
+        for s in range(N_UNITS + LAG_F + LAG_EXP + 1):
             b = s - LAG_F
             live = 2 <= b < N_UNITS
             crosses = [multiply_tile(b, h) for h in range(PAIR)] if live else []
@@ -270,10 +263,10 @@ def tile_rbf_t_kernel(tc, X, X2, lengthscale, variance, out):
                 g = b // 2
                 if g in FINE_GROUPS:
                     clamp_tiles(g, (b % 2) * PAIR, PAIR)
-                    waiting.append((s, g, (b % 2) * PAIR, PAIR))
+                    waiting.append((s + (g in GPSIMD_CLAMP_GROUPS), g, (b % 2) * PAIR, PAIR))
                 elif b % 2 == 1:
                     clamp_tiles(g, 0, TILES)
-                    waiting.append((s + (LAG_EXP_GPSIMD if g in GPSIMD_CLAMP_GROUPS else LAG_EXP_VECTOR), g, 0, TILES))
+                    waiting.append((s + LAG_EXP, g, 0, TILES))
             for due, g, first, count in sorted(waiting):
                 if due <= s:
                     finish_tiles(g, first, count)

@@ -1,4 +1,3 @@
-import math
 from contextlib import ExitStack
 
 import concourse.mybir as mybir
@@ -22,12 +21,17 @@ GROUP = P * TILES
 N_GROUPS = N_ROWS // GROUP + 1
 N_UNITS = 2 * N_GROUPS
 FLOPS = 2 * N_ROWS * M_ROWS * D_FEAT
-SQRT_HALF = math.sqrt(0.5)
 
-GPSIMD_CLAMP_GROUPS = tuple(range(1, 16))
-FINE_GROUPS = (15, 16)
-LAG_EXP = 1
+LEAD_T = 2
+LEAD_Q = 1
+LAG_S = 0
+LAG_D = 1
+LAG_B = 1
 LAG_F = 3
+LAG_EXP = 1
+VCLAMP = (33,)
+WIDE = ()
+BT, BS, BC = 3, 2, 3
 
 
 def tile_rbf_t_kernel(tc, X, X2, lengthscale, variance, out):
@@ -39,13 +43,13 @@ def tile_rbf_t_kernel(tc, X, X2, lengthscale, variance, out):
         stack.enter_context(tc.manual_schedule())
         const = stack.enter_context(tc.tile_pool(name="const", bufs=1))
         xin = stack.enter_context(tc.tile_pool(name="xin", bufs=N_GROUPS))
-        work = stack.enter_context(tc.tile_pool(name="work", bufs=3))
+        work = stack.enter_context(tc.tile_pool(name="work", bufs=4))
         held = stack.enter_context(tc.tile_pool(name="held", bufs=LAG_F + 3))
-        small = stack.enter_context(tc.tile_pool(name="small", bufs=4))
+        small = stack.enter_context(tc.tile_pool(name="small", bufs=8))
         outp = stack.enter_context(tc.tile_pool(name="outp", bufs=6))
-        psum_t = stack.enter_context(tc.psum_pool(name="psum_t", bufs=3))
-        psum_s = stack.enter_context(tc.psum_pool(name="psum_s", bufs=2))
-        psum_c = stack.enter_context(tc.psum_pool(name="psum_c", bufs=3))
+        psum_t = stack.enter_context(tc.psum_pool(name="psum_t", bufs=BT))
+        psum_s = stack.enter_context(tc.psum_pool(name="psum_s", bufs=BS))
+        psum_c = stack.enter_context(tc.psum_pool(name="psum_c", bufs=BC))
 
         raw = const.tile([P, 32], BF16, name="raw")
         one_col = const.tile([P, 1], F32, name="one_col")
@@ -72,7 +76,7 @@ def tile_rbf_t_kernel(tc, X, X2, lengthscale, variance, out):
         ident = const.tile([P, P], F32, name="ident")
         make_identity(nc, ident[:])
 
-        banks, squares, operands, sums, norms, results = {}, {}, {}, {}, {}, {}
+        banks, squares, scaled, operands, sums, norms, results = {}, {}, {}, {}, {}, {}, {}
 
         def transpose_unit(b):
             tb = psum_t.tile([P, 2 * UNIT], F32, name="tb")
@@ -85,8 +89,8 @@ def tile_rbf_t_kernel(tc, X, X2, lengthscale, variance, out):
                         ident[:],
                     )
 
-        transpose_unit(0)
-        transpose_unit(1)
+        for b in range(LEAD_T):
+            transpose_unit(b)
 
         W = 17
         absx = const.tile([P, W], F32, name="absx")
@@ -94,7 +98,7 @@ def tile_rbf_t_kernel(tc, X, X2, lengthscale, variance, out):
         logx = const.tile([P, W], F32, name="logx")
         soft = const.tile([P, W], F32, name="soft")
         invl = const.tile([P, PACK], F32, name="invl")
-        sinv = const.tile([P, PACK], F32, name="sinv")
+        halfw = const.tile([P, PACK], F32, name="halfw")
         lnv = const.tile([P, 1], F32, name="lnv")
         nc.scalar.activation(out=absx[:], in_=raw[:, 0:W], func=ACT.Abs)
         nc.scalar.activation(out=expx[:], in_=absx[:], func=ACT.Exp, scale=-1.0)
@@ -103,7 +107,9 @@ def tile_rbf_t_kernel(tc, X, X2, lengthscale, variance, out):
             out=soft[:], in0=raw[:, 0:W], scalar=0.0, in1=logx[:], op0=ALU.max, op1=ALU.add
         )
         nc.vector.reciprocal(out=invl[:], in_=soft[:, 0:PACK])
-        nc.vector.tensor_scalar(out=sinv[:], in0=invl[:], scalar1=SQRT_HALF, scalar2=None, op0=ALU.mult)
+        nc.vector.scalar_tensor_tensor(
+            out=halfw[:], in0=invl[:], scalar=0.5, in1=invl[:], op0=ALU.mult, op1=ALU.mult
+        )
         nc.scalar.activation(out=lnv[:], in_=soft[:, 16:17], func=ACT.Ln)
         invl_rep = invl[:].unsqueeze(1).to_broadcast([P, UNIT, PACK])
 
@@ -113,26 +119,24 @@ def tile_rbf_t_kernel(tc, X, X2, lengthscale, variance, out):
 
         def scale_unit(b):
             grouped = work.tile([P, UNIT, PACK], BF16, name="grouped", align_bytes=64)
+            scaled[b] = grouped
             nc.vector.tensor_tensor(
                 out=grouped[:].rearrange("p r (u e) -> p r u e", e=2),
                 in0=banks[b].rearrange("p (u r e) -> p r u e", u=2, e=2),
                 in1=invl_rep.rearrange("p r (u e) -> p r u e", e=2),
                 op=ALU.mult,
             )
-            return grouped
 
         def square_unit(b):
-            planes = banks[b].rearrange("p (u r e) -> p u e r", u=2, e=2)
             sq = work.tile([P, PACK, UNIT], F32, name="sq")
             squares[b] = sq
-            for u in range(2):
-                for e in range(2):
-                    t = 2 * u + e
-                    nc.scalar.activation(
-                        out=sq[:, t, :], in_=planes[:, u, e, :], func=ACT.Square, scale=sinv[:, t : t + 1]
-                    )
+            nc.scalar.activation(
+                out=sq[:].rearrange("p (u e) r -> p u e r", u=2),
+                in_=banks[b].rearrange("p (u r e) -> p u e r", u=2, e=2),
+                func=ACT.Square,
+            )
 
-        def quantise_unit(b, grouped):
+        def quantise_unit(b):
             if b < 2:
                 cols = slice(b * UNIT, (b + 1) * UNIT)
                 codes, scales = x2_codes[:, cols], x2_scales[:, cols]
@@ -142,38 +146,33 @@ def tile_rbf_t_kernel(tc, X, X2, lengthscale, variance, out):
                 codes, scales = codes_t[:], scales_t[:]
             operands[b] = (codes, scales)
             nc.vector.quantize_mx(
-                out=codes.bitcast(FP8X4), scales=scales, in_=grouped[:].rearrange("p r t -> p (r t)")
+                out=codes.bitcast(FP8X4), scales=scales, in_=scaled[b][:].rearrange("p r t -> p (r t)")
             )
 
         def sum_unit(b):
-            g = b // 2
-            if b % 2 == 0:
-                sums_t = psum_s.tile([P, TILES, P], F32, name="sums")
-                sums[g] = sums_t
+            sums_t = psum_s.tile([P, TILES, P], F32, name="sums")
+            sums[b] = sums_t
             for h in range(PAIR):
                 for t in range(PACK):
                     nc.tensor.matmul(
-                        out=sums[g][:, (b % 2) * PAIR + h, :],
+                        out=sums[b][:, 0, h : h + 1],
                         lhsT=squares[b][:, t, h * P : (h + 1) * P],
-                        rhs=ident[:],
-                        is_transpose=True,
+                        rhs=halfw[:, t : t + 1],
                         start=(t == 0),
                         stop=(t == PACK - 1),
                     )
 
-        def reduce_group(g):
-            norm = small.tile([P, TILES], F32, name="norm")
-            norms[g] = norm
-            for j in reversed(range(TILES)):
-                junk = work.tile([P, P], BF16, name="junk")
-                nc.scalar.activation(out=junk[:], in_=sums[g][:, j, :], func=ACT.Copy, accum_out=norm[:, j : j + 1])
+        def reduce_unit(b):
+            norm = small.tile([P, PAIR], F32, name="norm")
+            norms[b] = norm
+            nc.scalar.copy(out=norm[:], in_=sums[b][:, 0, 0:PAIR])
 
         def spread_column_norms():
             yn_ps = psum_s.tile([P, TILES, P], F32, name="sums")
             for j in range(TILES):
                 nc.tensor.matmul(
                     out=yn_ps[:, j, :],
-                    lhsT=norms[0][:, j : j + 1].to_broadcast([P, P]),
+                    lhsT=norms[j // PAIR][:, j % PAIR : j % PAIR + 1].to_broadcast([P, P]),
                     rhs=ident[:],
                     start=True,
                     stop=True,
@@ -210,63 +209,59 @@ def tile_rbf_t_kernel(tc, X, X2, lengthscale, variance, out):
             if g not in results:
                 res = outp.tile([P, TILES, M_ROWS], F32, name="res")
                 results[g] = res
+            row = results[g][:, j, :]
             nc.vector.scalar_tensor_tensor(
-                out=results[g][:, j, :],
-                in0=cross[:],
-                scalar=norms[g][:, j : j + 1],
-                in1=col_term[:],
-                op0=ALU.subtract,
-                op1=ALU.add,
+                out=row, in0=cross[:], scalar=norms[b][:, h : h + 1], in1=col_term[:], op0=ALU.subtract, op1=ALU.add
             )
-            if g in GPSIMD_CLAMP_GROUPS:
-                nc.gpsimd.tensor_scalar(
-                    out=results[g][:, j, :], in0=results[g][:, j, :],
-                    scalar1=0.0, scalar2=-1.0e30, op0=ALU.min, op1=ALU.max,
-                )
+            if b not in VCLAMP:
+                nc.gpsimd.tensor_scalar(out=row, in0=row, scalar1=0.0, scalar2=-1.0e30, op0=ALU.min, op1=ALU.max)
 
-        def clamp_tiles(g, first, count):
-            flat = results[g][:, first : first + count, :].rearrange("p j m -> p (j m)")
-            if g not in GPSIMD_CLAMP_GROUPS:
-                nc.vector.tensor_scalar(out=flat, in0=flat, scalar1=0.0, scalar2=None, op0=ALU.min)
+        def clamp_unit(b):
+            first = (b % 2) * PAIR
+            flat = results[b // 2][:, first : first + PAIR, :].rearrange("p j m -> p (j m)")
+            nc.vector.tensor_scalar(out=flat, in0=flat, scalar1=0.0, scalar2=None, op0=ALU.min)
 
         def finish_tiles(g, first, count):
             flat = results[g][:, first : first + count, :].rearrange("p j m -> p (j m)")
             nc.scalar.activation(out=flat, in_=flat, func=ACT.Exp, bias=lnv[:, 0:1])
             nc.sync.dma_start(out=out_view[g - 1][:, first * M_ROWS : (first + count) * M_ROWS], in_=flat)
 
-        square_unit(0)
+        for b in range(LEAD_Q):
+            square_unit(b)
         waiting = []
         yn_box = []
         for s in range(N_UNITS + LAG_F + LAG_EXP + 1):
             b = s - LAG_F
             live = 2 <= b < N_UNITS
             crosses = [multiply_tile(b, h) for h in range(PAIR)] if live else []
-            if s + 2 < N_UNITS:
-                transpose_unit(s + 2)
-            if s == 3:
+            if s + LEAD_T < N_UNITS:
+                transpose_unit(s + LEAD_T)
+            if s == 2 + LAG_D:
                 yn_box.append(spread_column_norms())
-            if s + 1 < N_UNITS:
-                square_unit(s + 1)
-            grouped = scale_unit(s) if s < N_UNITS else None
-            if s == 4:
-                negate_column_norms(yn_box[0])
+            if s + LEAD_Q < N_UNITS:
+                square_unit(s + LEAD_Q)
             if s < N_UNITS:
-                sum_unit(s)
-            if s % 2 == 0 and 0 <= (s - 2) // 2 < N_GROUPS and s >= 2:
-                reduce_group((s - 2) // 2)
+                scale_unit(s)
+            if s == 3 + LAG_D:
+                negate_column_norms(yn_box[0])
+            if 0 <= s - LAG_S < N_UNITS:
+                sum_unit(s - LAG_S)
+            if 0 <= s - LAG_D < N_UNITS:
+                reduce_unit(s - LAG_D)
             if live:
                 exponent_tile(b, 1, crosses[1])
-            if s < N_UNITS:
-                quantise_unit(s, grouped)
+            if 0 <= s - LAG_B < N_UNITS:
+                quantise_unit(s - LAG_B)
             if live:
                 exponent_tile(b, 0, crosses[0])
+                if b in VCLAMP:
+                    clamp_unit(b)
                 g = b // 2
-                if g in FINE_GROUPS:
-                    clamp_tiles(g, (b % 2) * PAIR, PAIR)
-                    waiting.append((s + (g in GPSIMD_CLAMP_GROUPS), g, (b % 2) * PAIR, PAIR))
-                elif b % 2 == 1:
-                    clamp_tiles(g, 0, TILES)
-                    waiting.append((s + LAG_EXP, g, 0, TILES))
+                if g in WIDE:
+                    if b % 2 == 1:
+                        waiting.append((s + LAG_EXP, g, 0, TILES))
+                else:
+                    waiting.append((s + (0 if b in VCLAMP else LAG_EXP), g, (b % 2) * PAIR, PAIR))
             for due, g, first, count in sorted(waiting):
                 if due <= s:
                     finish_tiles(g, first, count)

@@ -1,3 +1,4 @@
+import math
 from contextlib import ExitStack
 
 import concourse.mybir as mybir
@@ -10,8 +11,10 @@ U8 = mybir.dt.uint8
 FP8X4 = mybir.dt.float8_e4m3fn_x4
 ACT = mybir.ActivationFunctionType
 ALU = mybir.AluOpType
+AXIS = mybir.AxisListType
 
 P = 128
+W = 17
 N_ROWS, M_ROWS, D_FEAT = 8192, 512, 512
 PACK = 4
 TILES = 4
@@ -21,6 +24,7 @@ GROUP = P * TILES
 N_GROUPS = N_ROWS // GROUP + 1
 N_UNITS = 2 * N_GROUPS
 FLOPS = 2 * N_ROWS * M_ROWS * D_FEAT
+SQRT_HALF = math.sqrt(0.5)
 
 LEAD_T = 2
 LEAD_Q = 1
@@ -29,8 +33,9 @@ LAG_D = 1
 LAG_B = 1
 LAG_F = 3
 LAG_EXP = 1
-VCLAMP = (33,)
-WIDE = ()
+VRED = ()
+MMSUM = tuple(range(3, 34, 2))
+NCOL = 32
 BT, BS, BC = 3, 2, 3
 
 
@@ -54,14 +59,18 @@ def tile_rbf_t_kernel(tc, X, X2, lengthscale, variance, out):
         raw = const.tile([P, 32], BF16, name="raw")
         one_col = const.tile([P, 1], F32, name="one_col")
         warm = const.tile([P, 1], F32, name="warm")
+        base = const.tile([P, W], F32, name="base")
         nc.vector.memset(raw[:], 0.0)
         nc.vector.memset(one_col[:], 1.0)
+        nc.vector.tensor_scalar(
+            out=base[:], in0=one_col[:].to_broadcast([P, W]), scalar1=1.0 / math.e, scalar2=None, op0=ALU.mult
+        )
         nc.sync.dma_start(
             out=raw[:, 0:PACK].rearrange("p (u e) -> p u e", e=2),
             in_=lengthscale.rearrange("o (u p e) -> p (o u) e", p=P, e=2),
         )
         nc.sync.dma_start(out=raw[:, 16:17], in_=variance.partition_broadcast(P))
-        nc.scalar.activation(out=warm[:], in_=one_col[:], func=ACT.Exp)
+        nc.scalar.activation(out=warm[:], in_=one_col[:], func=ACT.Ln)
         sources = []
         for g in range(N_GROUPS):
             xg = xin.tile([P, TILES * D_FEAT], BF16, name="xg")
@@ -92,23 +101,29 @@ def tile_rbf_t_kernel(tc, X, X2, lengthscale, variance, out):
         for b in range(LEAD_T):
             transpose_unit(b)
 
-        W = 17
         absx = const.tile([P, W], F32, name="absx")
         expx = const.tile([P, W], F32, name="expx")
         logx = const.tile([P, W], F32, name="logx")
         soft = const.tile([P, W], F32, name="soft")
         invl = const.tile([P, PACK], F32, name="invl")
-        halfw = const.tile([P, PACK], F32, name="halfw")
+        sinv = const.tile([P, PACK], F32, name="sinv")
+        halfw = const.tile([P, PACK, NCOL], F32, name="halfw")
         lnv = const.tile([P, 1], F32, name="lnv")
-        nc.scalar.activation(out=absx[:], in_=raw[:, 0:W], func=ACT.Abs)
-        nc.scalar.activation(out=expx[:], in_=absx[:], func=ACT.Exp, scale=-1.0)
+        nc.vector.scalar_tensor_tensor(
+            out=absx[:], in0=raw[:, 0:W], scalar=-1.0, in1=raw[:, 0:W], op0=ALU.mult, op1=ALU.max
+        )
+        nc.gpsimd.tensor_tensor(out=expx[:], in0=base[:], in1=absx[:], op=ALU.pow)
         nc.scalar.activation(out=logx[:], in_=expx[:], func=ACT.Ln, bias=one_col[:, 0:1])
         nc.vector.scalar_tensor_tensor(
             out=soft[:], in0=raw[:, 0:W], scalar=0.0, in1=logx[:], op0=ALU.max, op1=ALU.add
         )
         nc.vector.reciprocal(out=invl[:], in_=soft[:, 0:PACK])
-        nc.vector.scalar_tensor_tensor(
-            out=halfw[:], in0=invl[:], scalar=0.5, in1=invl[:], op0=ALU.mult, op1=ALU.mult
+        nc.vector.tensor_scalar(out=sinv[:], in0=invl[:], scalar1=SQRT_HALF, scalar2=None, op0=ALU.mult)
+        nc.gpsimd.tensor_tensor(
+            out=halfw[:],
+            in0=sinv[:].unsqueeze(2).to_broadcast([P, PACK, NCOL]),
+            in1=sinv[:].unsqueeze(2).to_broadcast([P, PACK, NCOL]),
+            op=ALU.mult,
         )
         nc.scalar.activation(out=lnv[:], in_=soft[:, 16:17], func=ACT.Ln)
         invl_rep = invl[:].unsqueeze(1).to_broadcast([P, UNIT, PACK])
@@ -128,13 +143,18 @@ def tile_rbf_t_kernel(tc, X, X2, lengthscale, variance, out):
             )
 
         def square_unit(b):
+            planes = banks[b].rearrange("p (u r e) -> p u e r", u=2, e=2)
             sq = work.tile([P, PACK, UNIT], F32, name="sq")
             squares[b] = sq
-            nc.scalar.activation(
-                out=sq[:].rearrange("p (u e) r -> p u e r", u=2),
-                in_=banks[b].rearrange("p (u r e) -> p u e r", u=2, e=2),
-                func=ACT.Square,
-            )
+            if b in MMSUM:
+                nc.scalar.activation(out=sq[:].rearrange("p (u e) r -> p u e r", u=2), in_=planes, func=ACT.Square)
+                return
+            for u in range(2):
+                for e in range(2):
+                    t = 2 * u + e
+                    nc.scalar.activation(
+                        out=sq[:, t, :], in_=planes[:, u, e, :], func=ACT.Square, scale=sinv[:, t : t + 1]
+                    )
 
         def quantise_unit(b):
             if b < 2:
@@ -154,10 +174,20 @@ def tile_rbf_t_kernel(tc, X, X2, lengthscale, variance, out):
             sums[b] = sums_t
             for h in range(PAIR):
                 for t in range(PACK):
+                    if b in MMSUM:
+                        nc.tensor.matmul(
+                            out=sums[b][:, h, 0:NCOL],
+                            lhsT=squares[b][:, t, h * P : (h + 1) * P],
+                            rhs=halfw[:, t, :],
+                            start=(t == 0),
+                            stop=(t == PACK - 1),
+                        )
+                        continue
                     nc.tensor.matmul(
-                        out=sums[b][:, 0, h : h + 1],
+                        out=sums[b][:, h, :],
                         lhsT=squares[b][:, t, h * P : (h + 1) * P],
-                        rhs=halfw[:, t : t + 1],
+                        rhs=ident[:],
+                        is_transpose=True,
                         start=(t == 0),
                         stop=(t == PACK - 1),
                     )
@@ -165,7 +195,14 @@ def tile_rbf_t_kernel(tc, X, X2, lengthscale, variance, out):
         def reduce_unit(b):
             norm = small.tile([P, PAIR], F32, name="norm")
             norms[b] = norm
-            nc.scalar.copy(out=norm[:], in_=sums[b][:, 0, 0:PAIR])
+            if b in MMSUM:
+                nc.scalar.copy(out=norm[:], in_=sums[b][:, 0:PAIR, 0])
+            elif b in VRED:
+                nc.vector.tensor_reduce(out=norm[:], in_=sums[b][:, 0:PAIR, :], axis=AXIS.X, op=ALU.add)
+            else:
+                for h in reversed(range(PAIR)):
+                    junk = work.tile([P, P], BF16, name="junk")
+                    nc.scalar.activation(out=junk[:], in_=sums[b][:, h, :], func=ACT.Copy, accum_out=norm[:, h : h + 1])
 
         def spread_column_norms():
             yn_ps = psum_s.tile([P, TILES, P], F32, name="sums")
@@ -204,6 +241,7 @@ def tile_rbf_t_kernel(tc, X, X2, lengthscale, variance, out):
             return cross
 
         def exponent_tile(b, h, cross):
+            last = b == N_UNITS - 1
             g = b // 2
             j = (b % 2) * PAIR + h
             if g not in results:
@@ -213,22 +251,18 @@ def tile_rbf_t_kernel(tc, X, X2, lengthscale, variance, out):
             nc.vector.scalar_tensor_tensor(
                 out=row, in0=cross[:], scalar=norms[b][:, h : h + 1], in1=col_term[:], op0=ALU.subtract, op1=ALU.add
             )
-            if b not in VCLAMP:
+            if last:
+                nc.vector.tensor_scalar(out=row, in0=row, scalar1=0.0, scalar2=None, op0=ALU.min)
+                finish_tiles(g, j, 1)
+            else:
                 nc.gpsimd.tensor_scalar(out=row, in0=row, scalar1=0.0, scalar2=-1.0e30, op0=ALU.min, op1=ALU.max)
-
-        def clamp_unit(b):
-            first = (b % 2) * PAIR
-            flat = results[b // 2][:, first : first + PAIR, :].rearrange("p j m -> p (j m)")
-            nc.vector.tensor_scalar(out=flat, in0=flat, scalar1=0.0, scalar2=None, op0=ALU.min)
 
         def finish_tiles(g, first, count):
             flat = results[g][:, first : first + count, :].rearrange("p j m -> p (j m)")
             nc.scalar.activation(out=flat, in_=flat, func=ACT.Exp, bias=lnv[:, 0:1])
             nc.sync.dma_start(out=out_view[g - 1][:, first * M_ROWS : (first + count) * M_ROWS], in_=flat)
 
-        for b in range(LEAD_Q):
-            square_unit(b)
-        waiting = []
+        finish_list = []
         yn_box = []
         for s in range(N_UNITS + LAG_F + LAG_EXP + 1):
             b = s - LAG_F
@@ -236,33 +270,29 @@ def tile_rbf_t_kernel(tc, X, X2, lengthscale, variance, out):
             crosses = [multiply_tile(b, h) for h in range(PAIR)] if live else []
             if s + LEAD_T < N_UNITS:
                 transpose_unit(s + LEAD_T)
+            if 2 <= s - LAG_F - LAG_EXP < N_UNITS - 1:
+                done = s - LAG_F - LAG_EXP
+                finish_list.append((done // 2, (done % 2) * PAIR, PAIR))
             if s == 2 + LAG_D:
                 yn_box.append(spread_column_norms())
             if s + LEAD_Q < N_UNITS:
                 square_unit(s + LEAD_Q)
             if s < N_UNITS:
                 scale_unit(s)
+            if s == 0:
+                square_unit(0)
             if s == 3 + LAG_D:
                 negate_column_norms(yn_box[0])
             if 0 <= s - LAG_S < N_UNITS:
                 sum_unit(s - LAG_S)
             if 0 <= s - LAG_D < N_UNITS:
                 reduce_unit(s - LAG_D)
+            for entry in finish_list:
+                finish_tiles(*entry)
+            finish_list = []
             if live:
                 exponent_tile(b, 1, crosses[1])
             if 0 <= s - LAG_B < N_UNITS:
                 quantise_unit(s - LAG_B)
             if live:
                 exponent_tile(b, 0, crosses[0])
-                if b in VCLAMP:
-                    clamp_unit(b)
-                g = b // 2
-                if g in WIDE:
-                    if b % 2 == 1:
-                        waiting.append((s + LAG_EXP, g, 0, TILES))
-                else:
-                    waiting.append((s + (0 if b in VCLAMP else LAG_EXP), g, (b % 2) * PAIR, PAIR))
-            for due, g, first, count in sorted(waiting):
-                if due <= s:
-                    finish_tiles(g, first, count)
-            waiting = [entry for entry in waiting if entry[0] > s]

@@ -31,7 +31,7 @@ LEAD_Q = 1
 LAG_S = 0
 LAG_D = 1
 LAG_B = 1
-LAG_F = 3
+LAG_F = 2
 LAG_EXP = 1
 VRED = ()
 MMSUM = tuple(range(3, 34, 2))
@@ -59,18 +59,14 @@ def tile_rbf_t_kernel(tc, X, X2, lengthscale, variance, out):
         raw = const.tile([P, 32], BF16, name="raw")
         one_col = const.tile([P, 1], F32, name="one_col")
         warm = const.tile([P, 1], F32, name="warm")
-        base = const.tile([P, W], F32, name="base")
         nc.vector.memset(raw[:], 0.0)
         nc.vector.memset(one_col[:], 1.0)
-        nc.vector.tensor_scalar(
-            out=base[:], in0=one_col[:].to_broadcast([P, W]), scalar1=1.0 / math.e, scalar2=None, op0=ALU.mult
-        )
         nc.sync.dma_start(
             out=raw[:, 0:PACK].rearrange("p (u e) -> p u e", e=2),
             in_=lengthscale.rearrange("o (u p e) -> p (o u) e", p=P, e=2),
         )
         nc.sync.dma_start(out=raw[:, 16:17], in_=variance.partition_broadcast(P))
-        nc.scalar.activation(out=warm[:], in_=one_col[:], func=ACT.Ln)
+        nc.scalar.activation(out=warm[:], in_=one_col[:], func=ACT.Exp)
         sources = []
         for g in range(N_GROUPS):
             xg = xin.tile([P, TILES * D_FEAT], BF16, name="xg")
@@ -109,10 +105,8 @@ def tile_rbf_t_kernel(tc, X, X2, lengthscale, variance, out):
         sinv = const.tile([P, PACK], F32, name="sinv")
         halfw = const.tile([P, PACK, NCOL], F32, name="halfw")
         lnv = const.tile([P, 1], F32, name="lnv")
-        nc.vector.scalar_tensor_tensor(
-            out=absx[:], in0=raw[:, 0:W], scalar=-1.0, in1=raw[:, 0:W], op0=ALU.mult, op1=ALU.max
-        )
-        nc.gpsimd.tensor_tensor(out=expx[:], in0=base[:], in1=absx[:], op=ALU.pow)
+        nc.scalar.activation(out=absx[:], in_=raw[:, 0:W], func=ACT.Abs)
+        nc.scalar.activation(out=expx[:], in_=absx[:], func=ACT.Exp, scale=-1.0)
         nc.scalar.activation(out=logx[:], in_=expx[:], func=ACT.Ln, bias=one_col[:, 0:1])
         nc.vector.scalar_tensor_tensor(
             out=soft[:], in0=raw[:, 0:W], scalar=0.0, in1=logx[:], op0=ALU.max, op1=ALU.add

@@ -31,11 +31,14 @@ LEAD_Q = 1
 LAG_S = 0
 LAG_D = 1
 LAG_B = 1
-LAG_F = 2
+LAG_F = 3
 LAG_EXP = 1
-VRED = ()
-MMSUM = tuple(range(3, 34, 2))
-NCOL = 32
+VRED = tuple(range(3,34,4))
+MMSUM = ()
+NCOL = 4
+REPEATS = (1, 1)
+ORDER = "1B0"
+A_LATE = False
 BT, BS, BC = 3, 2, 3
 
 
@@ -51,7 +54,7 @@ def tile_rbf_t_kernel(tc, X, X2, lengthscale, variance, out):
         work = stack.enter_context(tc.tile_pool(name="work", bufs=4))
         held = stack.enter_context(tc.tile_pool(name="held", bufs=LAG_F + 3))
         small = stack.enter_context(tc.tile_pool(name="small", bufs=8))
-        outp = stack.enter_context(tc.tile_pool(name="outp", bufs=6))
+        outp = stack.enter_context(tc.tile_pool(name="outp", bufs=16))
         psum_t = stack.enter_context(tc.psum_pool(name="psum_t", bufs=BT))
         psum_s = stack.enter_context(tc.psum_pool(name="psum_s", bufs=BS))
         psum_c = stack.enter_context(tc.psum_pool(name="psum_c", bufs=BC))
@@ -59,14 +62,18 @@ def tile_rbf_t_kernel(tc, X, X2, lengthscale, variance, out):
         raw = const.tile([P, 32], BF16, name="raw")
         one_col = const.tile([P, 1], F32, name="one_col")
         warm = const.tile([P, 1], F32, name="warm")
+        base = const.tile([P, PACK], F32, name="base")
         nc.vector.memset(raw[:], 0.0)
         nc.vector.memset(one_col[:], 1.0)
+        nc.vector.tensor_scalar(
+            out=base[:], in0=one_col[:].to_broadcast([P, PACK]), scalar1=1.0 / math.e, scalar2=None, op0=ALU.mult
+        )
         nc.sync.dma_start(
             out=raw[:, 0:PACK].rearrange("p (u e) -> p u e", e=2),
             in_=lengthscale.rearrange("o (u p e) -> p (o u) e", p=P, e=2),
         )
         nc.sync.dma_start(out=raw[:, 16:17], in_=variance.partition_broadcast(P))
-        nc.scalar.activation(out=warm[:], in_=one_col[:], func=ACT.Exp)
+        nc.scalar.activation(out=warm[:], in_=one_col[:], func=ACT.Ln)
         sources = []
         for g in range(N_GROUPS):
             xg = xin.tile([P, TILES * D_FEAT], BF16, name="xg")
@@ -105,12 +112,21 @@ def tile_rbf_t_kernel(tc, X, X2, lengthscale, variance, out):
         sinv = const.tile([P, PACK], F32, name="sinv")
         halfw = const.tile([P, PACK, NCOL], F32, name="halfw")
         lnv = const.tile([P, 1], F32, name="lnv")
-        nc.scalar.activation(out=absx[:], in_=raw[:, 0:W], func=ACT.Abs)
-        nc.scalar.activation(out=expx[:], in_=absx[:], func=ACT.Exp, scale=-1.0)
-        nc.scalar.activation(out=logx[:], in_=expx[:], func=ACT.Ln, bias=one_col[:, 0:1])
-        nc.vector.scalar_tensor_tensor(
-            out=soft[:], in0=raw[:, 0:W], scalar=0.0, in1=logx[:], op0=ALU.max, op1=ALU.add
-        )
+
+        def softplus_front(cols, width):
+            nc.vector.scalar_tensor_tensor(
+                out=absx[:, cols], in0=raw[:, cols], scalar=-1.0, in1=raw[:, cols], op0=ALU.mult, op1=ALU.max
+            )
+            nc.gpsimd.tensor_tensor(out=expx[:, cols], in0=base[:, 0:width], in1=absx[:, cols], op=ALU.pow)
+            nc.scalar.activation(out=logx[:, cols], in_=expx[:, cols], func=ACT.Ln, bias=one_col[:, 0:1])
+
+        def softplus_back(cols):
+            nc.vector.scalar_tensor_tensor(
+                out=soft[:, cols], in0=raw[:, cols], scalar=0.0, in1=logx[:, cols], op0=ALU.max, op1=ALU.add
+            )
+
+        softplus_front(slice(0, PACK), PACK)
+        softplus_back(slice(0, PACK))
         nc.vector.reciprocal(out=invl[:], in_=soft[:, 0:PACK])
         nc.vector.tensor_scalar(out=sinv[:], in0=invl[:], scalar1=SQRT_HALF, scalar2=None, op0=ALU.mult)
         nc.gpsimd.tensor_tensor(
@@ -119,7 +135,6 @@ def tile_rbf_t_kernel(tc, X, X2, lengthscale, variance, out):
             in1=sinv[:].unsqueeze(2).to_broadcast([P, PACK, NCOL]),
             op=ALU.mult,
         )
-        nc.scalar.activation(out=lnv[:], in_=soft[:, 16:17], func=ACT.Ln)
         invl_rep = invl[:].unsqueeze(1).to_broadcast([P, UNIT, PACK])
 
         x2_codes = const.tile([P, M_ROWS], U32, name="x2_codes", align_bytes=64)
@@ -223,15 +238,16 @@ def tile_rbf_t_kernel(tc, X, X2, lengthscale, variance, out):
             codes, scales = operands[b]
             cols = slice(h * P, (h + 1) * P)
             cross = psum_c.tile([P, M_ROWS], F32, name="cross")
-            nc.tensor.matmul_mx(
-                out=cross[:],
-                lhsT=codes[:, cols].bitcast(FP8X4),
-                lhsT_scale=scales[:, cols],
-                rhs=x2_codes[:].bitcast(FP8X4),
-                rhs_scale=x2_scales[:],
-                start=True,
-                stop=True,
-            )
+            for repeat in range(REPEATS[h]):
+                nc.tensor.matmul_mx(
+                    out=cross[:],
+                    lhsT=codes[:, cols].bitcast(FP8X4),
+                    lhsT_scale=scales[:, cols],
+                    rhs=x2_codes[:].bitcast(FP8X4),
+                    rhs_scale=x2_scales[:],
+                    start=True,
+                    stop=True,
+                )
             return cross
 
         def exponent_tile(b, h, cross):
@@ -267,26 +283,34 @@ def tile_rbf_t_kernel(tc, X, X2, lengthscale, variance, out):
             if 2 <= s - LAG_F - LAG_EXP < N_UNITS - 1:
                 done = s - LAG_F - LAG_EXP
                 finish_list.append((done // 2, (done % 2) * PAIR, PAIR))
+            if s == 1:
+                softplus_front(slice(16, 17), 1)
+            if s == 2:
+                softplus_back(slice(16, 17))
+                nc.scalar.activation(out=lnv[:], in_=soft[:, 16:17], func=ACT.Ln)
             if s == 2 + LAG_D:
                 yn_box.append(spread_column_norms())
             if s + LEAD_Q < N_UNITS:
                 square_unit(s + LEAD_Q)
-            if s < N_UNITS:
+            if s < N_UNITS and not A_LATE:
                 scale_unit(s)
             if s == 0:
                 square_unit(0)
-            if s == 3 + LAG_D:
+            if s == 2 + LAG_D:
                 negate_column_norms(yn_box[0])
-            if 0 <= s - LAG_S < N_UNITS:
-                sum_unit(s - LAG_S)
             if 0 <= s - LAG_D < N_UNITS:
                 reduce_unit(s - LAG_D)
+            if 0 <= s - LAG_S < N_UNITS:
+                sum_unit(s - LAG_S)
             for entry in finish_list:
                 finish_tiles(*entry)
             finish_list = []
-            if live:
-                exponent_tile(b, 1, crosses[1])
-            if 0 <= s - LAG_B < N_UNITS:
-                quantise_unit(s - LAG_B)
-            if live:
-                exponent_tile(b, 0, crosses[0])
+            for tok in ORDER:
+                if tok == "1" and live:
+                    exponent_tile(b, 1, crosses[1])
+                if tok == "0" and live:
+                    exponent_tile(b, 0, crosses[0])
+                if tok == "B" and 0 <= s - LAG_B < N_UNITS:
+                    quantise_unit(s - LAG_B)
+                if tok == "A" and A_LATE and s < N_UNITS:
+                    scale_unit(s)

@@ -33,9 +33,12 @@ LAG_D = 1
 LAG_B = 1
 LAG_F = 3
 LAG_EXP = 1
-VRED = tuple(range(3,34,4))
+VRED = ()
 MMSUM = ()
-NCOL = 4
+NCOL = 32
+WIDE_B = True
+FLIP = 0
+EXIT_TILES = ()
 REPEATS = (1, 1)
 ORDER = "1B0"
 A_LATE = False
@@ -52,7 +55,8 @@ def tile_rbf_t_kernel(tc, X, X2, lengthscale, variance, out):
         const = stack.enter_context(tc.tile_pool(name="const", bufs=1))
         xin = stack.enter_context(tc.tile_pool(name="xin", bufs=N_GROUPS))
         work = stack.enter_context(tc.tile_pool(name="work", bufs=4))
-        held = stack.enter_context(tc.tile_pool(name="held", bufs=LAG_F + 3))
+        pairs = stack.enter_context(tc.tile_pool(name="pairs", bufs=2))
+        held = stack.enter_context(tc.tile_pool(name="held", bufs=(LAG_F + 3) // (2 if WIDE_B else 1)))
         small = stack.enter_context(tc.tile_pool(name="small", bufs=8))
         outp = stack.enter_context(tc.tile_pool(name="outp", bufs=16))
         psum_t = stack.enter_context(tc.psum_pool(name="psum_t", bufs=BT))
@@ -142,10 +146,14 @@ def tile_rbf_t_kernel(tc, X, X2, lengthscale, variance, out):
         col_term = const.tile([P, M_ROWS], F32, name="col_term")
 
         def scale_unit(b):
-            grouped = work.tile([P, UNIT, PACK], BF16, name="grouped", align_bytes=64)
+            if WIDE_B and b % 2 == 1:
+                grouped = scaled[b - 1]
+            else:
+                grouped = pairs.tile([P, (2 if WIDE_B else 1) * UNIT, PACK], BF16, name="grouped", align_bytes=64)
             scaled[b] = grouped
+            half = (b % 2) * UNIT if WIDE_B else 0
             nc.vector.tensor_tensor(
-                out=grouped[:].rearrange("p r (u e) -> p r u e", e=2),
+                out=grouped[:, half : half + UNIT, :].rearrange("p r (u e) -> p r u e", e=2),
                 in0=banks[b].rearrange("p (u r e) -> p r u e", u=2, e=2),
                 in1=invl_rep.rearrange("p r (u e) -> p r u e", e=2),
                 op=ALU.mult,
@@ -166,6 +174,21 @@ def tile_rbf_t_kernel(tc, X, X2, lengthscale, variance, out):
                     )
 
         def quantise_unit(b):
+            if WIDE_B and b % 2 == 0:
+                return
+            if WIDE_B:
+                if b < 2:
+                    codes, scales = x2_codes[:], x2_scales[:]
+                else:
+                    codes_t = held.tile([P, 2 * UNIT], U32, name="codes", align_bytes=64)
+                    scales_t = held.tile([P, 2 * UNIT], U8, name="scales", align_bytes=64)
+                    codes, scales = codes_t[:], scales_t[:]
+                operands[b - 1] = (codes[:, 0:UNIT], scales[:, 0:UNIT])
+                operands[b] = (codes[:, UNIT : 2 * UNIT], scales[:, UNIT : 2 * UNIT])
+                nc.vector.quantize_mx(
+                    out=codes.bitcast(FP8X4), scales=scales, in_=scaled[b][:].rearrange("p r t -> p (r t)")
+                )
+                return
             if b < 2:
                 cols = slice(b * UNIT, (b + 1) * UNIT)
                 codes, scales = x2_codes[:, cols], x2_scales[:, cols]
@@ -258,6 +281,15 @@ def tile_rbf_t_kernel(tc, X, X2, lengthscale, variance, out):
                 res = outp.tile([P, TILES, M_ROWS], F32, name="res")
                 results[g] = res
             row = results[g][:, j, :]
+            if (b, h) in EXIT_TILES:
+                nc.scalar.activation(out=row, in_=cross[:], func=ACT.Identity, scale=-1.0, bias=norms[b][:, h : h + 1])
+                for c in range(2):
+                    cols = slice(c * M_ROWS // 2, (c + 1) * M_ROWS // 2)
+                    nc.gpsimd.tensor_tensor(
+                        out=row[:, cols], in0=col_term[:, cols], in1=row[:, cols], op=ALU.subtract
+                    )
+                nc.gpsimd.tensor_scalar(out=row, in0=row, scalar1=0.0, scalar2=-1.0e30, op0=ALU.min, op1=ALU.max)
+                return
             nc.vector.scalar_tensor_tensor(
                 out=row, in0=cross[:], scalar=norms[b][:, h : h + 1], in1=col_term[:], op0=ALU.subtract, op1=ALU.add
             )
@@ -277,7 +309,10 @@ def tile_rbf_t_kernel(tc, X, X2, lengthscale, variance, out):
         for s in range(N_UNITS + LAG_F + LAG_EXP + 1):
             b = s - LAG_F
             live = 2 <= b < N_UNITS
-            crosses = [multiply_tile(b, h) for h in range(PAIR)] if live else []
+            crosses = {}
+            if live:
+                for h in ((1, 0) if s >= FLIP else (0, 1)):
+                    crosses[h] = multiply_tile(b, h)
             if s + LEAD_T < N_UNITS:
                 transpose_unit(s + LEAD_T)
             if 2 <= s - LAG_F - LAG_EXP < N_UNITS - 1:
@@ -296,7 +331,7 @@ def tile_rbf_t_kernel(tc, X, X2, lengthscale, variance, out):
                 scale_unit(s)
             if s == 0:
                 square_unit(0)
-            if s == 2 + LAG_D:
+            if s == 3 + LAG_D:
                 negate_column_norms(yn_box[0])
             if 0 <= s - LAG_D < N_UNITS:
                 reduce_unit(s - LAG_D)

@@ -14,35 +14,21 @@ ALU = mybir.AluOpType
 AXIS = mybir.AxisListType
 
 P = 128
-W = 17
 N_ROWS, M_ROWS, D_FEAT = 8192, 512, 512
 PACK = 4
 TILES = 4
 PAIR = 2
 UNIT = PAIR * P
-GROUP = P * TILES
+GROUP = TILES * P
 N_GROUPS = N_ROWS // GROUP + 1
 N_UNITS = 2 * N_GROUPS
 FLOPS = 2 * N_ROWS * M_ROWS * D_FEAT
 SQRT_HALF = math.sqrt(0.5)
 
-LEAD_T = 2
-LEAD_Q = 1
-LAG_S = 0
-LAG_D = 1
-LAG_B = 1
-LAG_F = 3
-LAG_EXP = 1
-VRED = ()
-MMSUM = ()
-NCOL = 32
-WIDE_B = True
-FLIP = 0
-EXIT_TILES = ()
-REPEATS = (1, 1)
-ORDER = "1B0"
-A_LATE = False
-BT, BS, BC = 3, 2, 3
+VAR_COL = 16
+LAG_MULTIPLY = 3
+LAG_EXP = 2
+VECTOR_SUMS = tuple(range(6, N_UNITS, 6))
 
 
 def tile_rbf_t_kernel(tc, X, X2, lengthscale, variance, out):
@@ -56,12 +42,12 @@ def tile_rbf_t_kernel(tc, X, X2, lengthscale, variance, out):
         xin = stack.enter_context(tc.tile_pool(name="xin", bufs=N_GROUPS))
         work = stack.enter_context(tc.tile_pool(name="work", bufs=4))
         pairs = stack.enter_context(tc.tile_pool(name="pairs", bufs=2))
-        held = stack.enter_context(tc.tile_pool(name="held", bufs=(LAG_F + 3) // (2 if WIDE_B else 1)))
+        held = stack.enter_context(tc.tile_pool(name="held", bufs=3))
         small = stack.enter_context(tc.tile_pool(name="small", bufs=8))
-        outp = stack.enter_context(tc.tile_pool(name="outp", bufs=16))
-        psum_t = stack.enter_context(tc.psum_pool(name="psum_t", bufs=BT))
-        psum_s = stack.enter_context(tc.psum_pool(name="psum_s", bufs=BS))
-        psum_c = stack.enter_context(tc.psum_pool(name="psum_c", bufs=BC))
+        outp = stack.enter_context(tc.tile_pool(name="outp", bufs=N_GROUPS - 1))
+        psum_t = stack.enter_context(tc.psum_pool(name="psum_t", bufs=3))
+        psum_s = stack.enter_context(tc.psum_pool(name="psum_s", bufs=2))
+        psum_c = stack.enter_context(tc.psum_pool(name="psum_c", bufs=3))
 
         raw = const.tile([P, 32], BF16, name="raw")
         one_col = const.tile([P, 1], F32, name="one_col")
@@ -76,9 +62,9 @@ def tile_rbf_t_kernel(tc, X, X2, lengthscale, variance, out):
             out=raw[:, 0:PACK].rearrange("p (u e) -> p u e", e=2),
             in_=lengthscale.rearrange("o (u p e) -> p (o u) e", p=P, e=2),
         )
-        nc.sync.dma_start(out=raw[:, 16:17], in_=variance.partition_broadcast(P))
+        nc.sync.dma_start(out=raw[:, VAR_COL : VAR_COL + 1], in_=variance.partition_broadcast(P))
         nc.scalar.activation(out=warm[:], in_=one_col[:], func=ACT.Ln)
-        sources = []
+        words = []
         for g in range(N_GROUPS):
             xg = xin.tile([P, TILES * D_FEAT], BF16, name="xg")
             if g == 0:
@@ -87,134 +73,100 @@ def tile_rbf_t_kernel(tc, X, X2, lengthscale, variance, out):
                 )
             else:
                 nc.sync.dma_start(out=xg[:], in_=x_view[g - 1])
-            sources.append(xg[:].bitcast(F32).rearrange("p (j w) -> p j w", j=TILES))
+            words.append(xg[:].bitcast(F32).rearrange("p (j w) -> p j w", j=TILES))
 
         ident = const.tile([P, P], F32, name="ident")
         make_identity(nc, ident[:])
 
-        banks, squares, scaled, operands, sums, norms, results = {}, {}, {}, {}, {}, {}, {}
+        banks, squares, sums, norms, operands, scaled, results = {}, {}, {}, {}, {}, {}, {}
 
         def transpose_unit(b):
-            tb = psum_t.tile([P, 2 * UNIT], F32, name="tb")
-            banks[b] = tb[:].bitcast(BF16)
+            bank = psum_t.tile([P, 2 * UNIT], F32, name="bank")
+            banks[b] = bank[:].bitcast(BF16)
             for u in range(2):
                 for h in range(PAIR):
                     nc.tensor.transpose(
-                        tb[:, (u * PAIR + h) * P : (u * PAIR + h + 1) * P],
-                        sources[b // 2][:, (b % 2) * PAIR + h, u * P : (u + 1) * P],
+                        bank[:, (u * PAIR + h) * P : (u * PAIR + h + 1) * P],
+                        words[b // 2][:, (b % 2) * PAIR + h, u * P : (u + 1) * P],
                         ident[:],
                     )
 
-        for b in range(LEAD_T):
-            transpose_unit(b)
+        transpose_unit(0)
+        transpose_unit(1)
 
-        absx = const.tile([P, W], F32, name="absx")
-        expx = const.tile([P, W], F32, name="expx")
-        logx = const.tile([P, W], F32, name="logx")
-        soft = const.tile([P, W], F32, name="soft")
+        absx = const.tile([P, VAR_COL + 1], F32, name="absx")
+        expx = const.tile([P, VAR_COL + 1], F32, name="expx")
+        logx = const.tile([P, VAR_COL + 1], F32, name="logx")
+        soft = const.tile([P, VAR_COL + 1], F32, name="soft")
         invl = const.tile([P, PACK], F32, name="invl")
         sinv = const.tile([P, PACK], F32, name="sinv")
-        halfw = const.tile([P, PACK, NCOL], F32, name="halfw")
         lnv = const.tile([P, 1], F32, name="lnv")
 
-        def softplus_front(cols, width):
+        def softplus_log(cols, width):
             nc.vector.scalar_tensor_tensor(
                 out=absx[:, cols], in0=raw[:, cols], scalar=-1.0, in1=raw[:, cols], op0=ALU.mult, op1=ALU.max
             )
             nc.gpsimd.tensor_tensor(out=expx[:, cols], in0=base[:, 0:width], in1=absx[:, cols], op=ALU.pow)
             nc.scalar.activation(out=logx[:, cols], in_=expx[:, cols], func=ACT.Ln, bias=one_col[:, 0:1])
 
-        def softplus_back(cols):
+        def softplus_sum(cols):
             nc.vector.scalar_tensor_tensor(
                 out=soft[:, cols], in0=raw[:, cols], scalar=0.0, in1=logx[:, cols], op0=ALU.max, op1=ALU.add
             )
 
-        softplus_front(slice(0, PACK), PACK)
-        softplus_back(slice(0, PACK))
+        softplus_log(slice(0, PACK), PACK)
+        softplus_sum(slice(0, PACK))
         nc.vector.reciprocal(out=invl[:], in_=soft[:, 0:PACK])
         nc.vector.tensor_scalar(out=sinv[:], in0=invl[:], scalar1=SQRT_HALF, scalar2=None, op0=ALU.mult)
-        nc.gpsimd.tensor_tensor(
-            out=halfw[:],
-            in0=sinv[:].unsqueeze(2).to_broadcast([P, PACK, NCOL]),
-            in1=sinv[:].unsqueeze(2).to_broadcast([P, PACK, NCOL]),
-            op=ALU.mult,
-        )
         invl_rep = invl[:].unsqueeze(1).to_broadcast([P, UNIT, PACK])
+        var_col = slice(VAR_COL, VAR_COL + 1)
 
         x2_codes = const.tile([P, M_ROWS], U32, name="x2_codes", align_bytes=64)
         x2_scales = const.tile([P, M_ROWS], U8, name="x2_scales", align_bytes=64)
         col_term = const.tile([P, M_ROWS], F32, name="col_term")
 
         def scale_unit(b):
-            if WIDE_B and b % 2 == 1:
-                grouped = scaled[b - 1]
-            else:
-                grouped = pairs.tile([P, (2 if WIDE_B else 1) * UNIT, PACK], BF16, name="grouped", align_bytes=64)
-            scaled[b] = grouped
-            half = (b % 2) * UNIT if WIDE_B else 0
+            if b % 2 == 0:
+                grouped = pairs.tile([P, GROUP, PACK], BF16, name="grouped", align_bytes=64)
+                scaled[b // 2] = grouped
+            rows = slice((b % 2) * UNIT, (b % 2 + 1) * UNIT)
             nc.vector.tensor_tensor(
-                out=grouped[:, half : half + UNIT, :].rearrange("p r (u e) -> p r u e", e=2),
+                out=scaled[b // 2][:, rows, :].rearrange("p r (u e) -> p r u e", e=2),
                 in0=banks[b].rearrange("p (u r e) -> p r u e", u=2, e=2),
                 in1=invl_rep.rearrange("p r (u e) -> p r u e", e=2),
                 op=ALU.mult,
             )
 
         def square_unit(b):
-            planes = banks[b].rearrange("p (u r e) -> p u e r", u=2, e=2)
+            slots = banks[b].rearrange("p (u r e) -> p u e r", u=2, e=2)
             sq = work.tile([P, PACK, UNIT], F32, name="sq")
             squares[b] = sq
-            if b in MMSUM:
-                nc.scalar.activation(out=sq[:].rearrange("p (u e) r -> p u e r", u=2), in_=planes, func=ACT.Square)
-                return
             for u in range(2):
                 for e in range(2):
                     t = 2 * u + e
                     nc.scalar.activation(
-                        out=sq[:, t, :], in_=planes[:, u, e, :], func=ACT.Square, scale=sinv[:, t : t + 1]
+                        out=sq[:, t, :], in_=slots[:, u, e, :], func=ACT.Square, scale=sinv[:, t : t + 1]
                     )
 
-        def quantise_unit(b):
-            if WIDE_B and b % 2 == 0:
-                return
-            if WIDE_B:
-                if b < 2:
-                    codes, scales = x2_codes[:], x2_scales[:]
-                else:
-                    codes_t = held.tile([P, 2 * UNIT], U32, name="codes", align_bytes=64)
-                    scales_t = held.tile([P, 2 * UNIT], U8, name="scales", align_bytes=64)
-                    codes, scales = codes_t[:], scales_t[:]
-                operands[b - 1] = (codes[:, 0:UNIT], scales[:, 0:UNIT])
-                operands[b] = (codes[:, UNIT : 2 * UNIT], scales[:, UNIT : 2 * UNIT])
-                nc.vector.quantize_mx(
-                    out=codes.bitcast(FP8X4), scales=scales, in_=scaled[b][:].rearrange("p r t -> p (r t)")
-                )
-                return
-            if b < 2:
-                cols = slice(b * UNIT, (b + 1) * UNIT)
-                codes, scales = x2_codes[:, cols], x2_scales[:, cols]
+        def quantise_group(g):
+            if g == 0:
+                codes, scales = x2_codes[:], x2_scales[:]
             else:
-                codes_t = held.tile([P, UNIT], U32, name="codes", align_bytes=64)
-                scales_t = held.tile([P, UNIT], U8, name="scales", align_bytes=64)
+                codes_t = held.tile([P, GROUP], U32, name="codes", align_bytes=64)
+                scales_t = held.tile([P, GROUP], U8, name="scales", align_bytes=64)
                 codes, scales = codes_t[:], scales_t[:]
-            operands[b] = (codes, scales)
             nc.vector.quantize_mx(
-                out=codes.bitcast(FP8X4), scales=scales, in_=scaled[b][:].rearrange("p r t -> p (r t)")
+                out=codes.bitcast(FP8X4), scales=scales, in_=scaled[g][:].rearrange("p r t -> p (r t)")
             )
+            for b in (2 * g, 2 * g + 1):
+                rows = slice((b % 2) * UNIT, (b % 2 + 1) * UNIT)
+                operands[b] = (codes[:, rows], scales[:, rows])
 
         def sum_unit(b):
             sums_t = psum_s.tile([P, TILES, P], F32, name="sums")
             sums[b] = sums_t
             for h in range(PAIR):
                 for t in range(PACK):
-                    if b in MMSUM:
-                        nc.tensor.matmul(
-                            out=sums[b][:, h, 0:NCOL],
-                            lhsT=squares[b][:, t, h * P : (h + 1) * P],
-                            rhs=halfw[:, t, :],
-                            start=(t == 0),
-                            stop=(t == PACK - 1),
-                        )
-                        continue
                     nc.tensor.matmul(
                         out=sums[b][:, h, :],
                         lhsT=squares[b][:, t, h * P : (h + 1) * P],
@@ -227,9 +179,7 @@ def tile_rbf_t_kernel(tc, X, X2, lengthscale, variance, out):
         def reduce_unit(b):
             norm = small.tile([P, PAIR], F32, name="norm")
             norms[b] = norm
-            if b in MMSUM:
-                nc.scalar.copy(out=norm[:], in_=sums[b][:, 0:PAIR, 0])
-            elif b in VRED:
+            if b in VECTOR_SUMS:
                 nc.vector.tensor_reduce(out=norm[:], in_=sums[b][:, 0:PAIR, :], axis=AXIS.X, op=ALU.add)
             else:
                 for h in reversed(range(PAIR)):
@@ -248,104 +198,78 @@ def tile_rbf_t_kernel(tc, X, X2, lengthscale, variance, out):
                 )
             return yn_ps
 
-        def negate_column_norms(yn_ps):
-            nc.vector.tensor_scalar(
-                out=col_term[:],
-                in0=yn_ps[:].rearrange("p j r -> p (j r)"),
-                scalar1=-1.0,
-                scalar2=None,
-                op0=ALU.mult,
-            )
-
         def multiply_tile(b, h):
             codes, scales = operands[b]
             cols = slice(h * P, (h + 1) * P)
             cross = psum_c.tile([P, M_ROWS], F32, name="cross")
-            for repeat in range(REPEATS[h]):
-                nc.tensor.matmul_mx(
-                    out=cross[:],
-                    lhsT=codes[:, cols].bitcast(FP8X4),
-                    lhsT_scale=scales[:, cols],
-                    rhs=x2_codes[:].bitcast(FP8X4),
-                    rhs_scale=x2_scales[:],
-                    start=True,
-                    stop=True,
-                )
-            return cross
-
-        def exponent_tile(b, h, cross):
-            last = b == N_UNITS - 1
-            g = b // 2
-            j = (b % 2) * PAIR + h
-            if g not in results:
-                res = outp.tile([P, TILES, M_ROWS], F32, name="res")
-                results[g] = res
-            row = results[g][:, j, :]
-            if (b, h) in EXIT_TILES:
-                nc.scalar.activation(out=row, in_=cross[:], func=ACT.Identity, scale=-1.0, bias=norms[b][:, h : h + 1])
-                for c in range(2):
-                    cols = slice(c * M_ROWS // 2, (c + 1) * M_ROWS // 2)
-                    nc.gpsimd.tensor_tensor(
-                        out=row[:, cols], in0=col_term[:, cols], in1=row[:, cols], op=ALU.subtract
-                    )
-                nc.gpsimd.tensor_scalar(out=row, in0=row, scalar1=0.0, scalar2=-1.0e30, op0=ALU.min, op1=ALU.max)
-                return
-            nc.vector.scalar_tensor_tensor(
-                out=row, in0=cross[:], scalar=norms[b][:, h : h + 1], in1=col_term[:], op0=ALU.subtract, op1=ALU.add
+            nc.tensor.matmul_mx(
+                out=cross[:],
+                lhsT=codes[:, cols].bitcast(FP8X4),
+                lhsT_scale=scales[:, cols],
+                rhs=x2_codes[:].bitcast(FP8X4),
+                rhs_scale=x2_scales[:],
+                start=True,
+                stop=True,
             )
-            if last:
-                nc.vector.tensor_scalar(out=row, in0=row, scalar1=0.0, scalar2=None, op0=ALU.min)
-                finish_tiles(g, j, 1)
-            else:
-                nc.gpsimd.tensor_scalar(out=row, in0=row, scalar1=0.0, scalar2=-1.0e30, op0=ALU.min, op1=ALU.max)
+            return cross
 
         def finish_tiles(g, first, count):
             flat = results[g][:, first : first + count, :].rearrange("p j m -> p (j m)")
             nc.scalar.activation(out=flat, in_=flat, func=ACT.Exp, bias=lnv[:, 0:1])
             nc.sync.dma_start(out=out_view[g - 1][:, first * M_ROWS : (first + count) * M_ROWS], in_=flat)
 
-        finish_list = []
-        yn_box = []
-        for s in range(N_UNITS + LAG_F + LAG_EXP + 1):
-            b = s - LAG_F
-            live = 2 <= b < N_UNITS
+        def exponent_tile(b, h, cross):
+            g, j = b // 2, (b % 2) * PAIR + h
+            if g not in results:
+                res = outp.tile([P, TILES, M_ROWS], F32, name="res")
+                results[g] = res
+            row = results[g][:, j, :]
+            nc.vector.scalar_tensor_tensor(
+                out=row, in0=cross[:], scalar=norms[b][:, h : h + 1], in1=col_term[:], op0=ALU.subtract, op1=ALU.add
+            )
+            if b == N_UNITS - 1:
+                nc.vector.tensor_scalar(out=row, in0=row, scalar1=0.0, scalar2=None, op0=ALU.min)
+                finish_tiles(g, j, 1)
+            else:
+                nc.gpsimd.tensor_scalar(out=row, in0=row, scalar1=0.0, scalar2=-1.0e30, op0=ALU.min, op1=ALU.max)
+
+        yn_ps = None
+        for s in range(N_UNITS + LAG_MULTIPLY):
+            b = s - LAG_MULTIPLY
+            live = b >= 2
             crosses = {}
             if live:
-                for h in ((1, 0) if s >= FLIP else (0, 1)):
+                for h in reversed(range(PAIR)):
                     crosses[h] = multiply_tile(b, h)
-            if s + LEAD_T < N_UNITS:
-                transpose_unit(s + LEAD_T)
-            if 2 <= s - LAG_F - LAG_EXP < N_UNITS - 1:
-                done = s - LAG_F - LAG_EXP
-                finish_list.append((done // 2, (done % 2) * PAIR, PAIR))
+            if s + 2 < N_UNITS:
+                transpose_unit(s + 2)
             if s == 1:
-                softplus_front(slice(16, 17), 1)
+                softplus_log(var_col, 1)
             if s == 2:
-                softplus_back(slice(16, 17))
-                nc.scalar.activation(out=lnv[:], in_=soft[:, 16:17], func=ACT.Ln)
-            if s == 2 + LAG_D:
-                yn_box.append(spread_column_norms())
-            if s + LEAD_Q < N_UNITS:
-                square_unit(s + LEAD_Q)
-            if s < N_UNITS and not A_LATE:
+                softplus_sum(var_col)
+                nc.scalar.activation(out=lnv[:], in_=soft[:, var_col], func=ACT.Ln)
+            if s == 3:
+                yn_ps = spread_column_norms()
+            if s + 1 < N_UNITS:
+                square_unit(s + 1)
+            if s < N_UNITS:
                 scale_unit(s)
             if s == 0:
                 square_unit(0)
-            if s == 3 + LAG_D:
-                negate_column_norms(yn_box[0])
-            if 0 <= s - LAG_D < N_UNITS:
-                reduce_unit(s - LAG_D)
-            if 0 <= s - LAG_S < N_UNITS:
-                sum_unit(s - LAG_S)
-            for entry in finish_list:
-                finish_tiles(*entry)
-            finish_list = []
-            for tok in ORDER:
-                if tok == "1" and live:
-                    exponent_tile(b, 1, crosses[1])
-                if tok == "0" and live:
-                    exponent_tile(b, 0, crosses[0])
-                if tok == "B" and 0 <= s - LAG_B < N_UNITS:
-                    quantise_unit(s - LAG_B)
-                if tok == "A" and A_LATE and s < N_UNITS:
-                    scale_unit(s)
+            if s == 4:
+                nc.vector.tensor_scalar(
+                    out=col_term[:], in0=yn_ps[:].rearrange("p j r -> p (j r)"), scalar1=-1.0, scalar2=None, op0=ALU.mult
+                )
+            if s < N_UNITS:
+                sum_unit(s)
+            if 1 <= s <= N_UNITS:
+                reduce_unit(s - 1)
+            for done in range(2, N_UNITS - 1):
+                if b - done == (LAG_EXP if done < N_UNITS - 2 else 1):
+                    finish_tiles(done // 2, (done % 2) * PAIR, PAIR)
+            if live:
+                exponent_tile(b, 1, crosses[1])
+            if s % 2 == 0 and 2 <= s <= N_UNITS:
+                quantise_group(s // 2 - 1)
+            if live:
+                exponent_tile(b, 0, crosses[0])

import math
from contextlib import ExitStack

import concourse.mybir as mybir
from concourse.masks import make_identity

F32 = mybir.dt.float32
BF16 = mybir.dt.bfloat16
U32 = mybir.dt.uint32
U8 = mybir.dt.uint8
FP8X4 = mybir.dt.float8_e4m3fn_x4
ACT = mybir.ActivationFunctionType
ALU = mybir.AluOpType
AXIS = mybir.AxisListType

P = 128
N_ROWS, M_ROWS, D_FEAT = 8192, 512, 512
PACK = 4
TILES = 4
PAIR = 2
UNIT = PAIR * P
GROUP = TILES * P
N_GROUPS = N_ROWS // GROUP + 1
N_UNITS = 2 * N_GROUPS
FLOPS = 2 * N_ROWS * M_ROWS * D_FEAT
SQRT_HALF = math.sqrt(0.5)

VAR_COL = 16
LAG_MULTIPLY = 3
LAG_EXP = 2
VECTOR_SUMS = tuple(range(6, N_UNITS, 6))


def tile_rbf_t_kernel(tc, X, X2, lengthscale, variance, out):
    nc = tc.nc
    x_view = X.rearrange("(g p j) k -> g p (j k)", p=P, j=TILES)
    out_view = out.rearrange("(g p j) m -> g p (j m)", p=P, j=TILES)

    with ExitStack() as stack:
        stack.enter_context(tc.manual_schedule())
        const = stack.enter_context(tc.tile_pool(name="const", bufs=1))
        xin = stack.enter_context(tc.tile_pool(name="xin", bufs=N_GROUPS))
        work = stack.enter_context(tc.tile_pool(name="work", bufs=4))
        pairs = stack.enter_context(tc.tile_pool(name="pairs", bufs=2))
        held = stack.enter_context(tc.tile_pool(name="held", bufs=3))
        small = stack.enter_context(tc.tile_pool(name="small", bufs=8))
        outp = stack.enter_context(tc.tile_pool(name="outp", bufs=N_GROUPS - 1))
        psum_t = stack.enter_context(tc.psum_pool(name="psum_t", bufs=3))
        psum_s = stack.enter_context(tc.psum_pool(name="psum_s", bufs=2))
        psum_c = stack.enter_context(tc.psum_pool(name="psum_c", bufs=3))

        raw = const.tile([P, 32], BF16, name="raw")
        one_col = const.tile([P, 1], F32, name="one_col")
        warm = const.tile([P, 1], F32, name="warm")
        base = const.tile([P, PACK], F32, name="base")
        nc.vector.memset(raw[:], 0.0)
        nc.vector.memset(one_col[:], 1.0)
        nc.vector.tensor_scalar(
            out=base[:], in0=one_col[:].to_broadcast([P, PACK]), scalar1=1.0 / math.e, scalar2=None, op0=ALU.mult
        )
        nc.sync.dma_start(
            out=raw[:, 0:PACK].rearrange("p (u e) -> p u e", e=2),
            in_=lengthscale.rearrange("o (u p e) -> p (o u) e", p=P, e=2),
        )
        nc.sync.dma_start(out=raw[:, VAR_COL : VAR_COL + 1], in_=variance.partition_broadcast(P))
        nc.scalar.activation(out=warm[:], in_=one_col[:], func=ACT.Ln)
        words = []
        for g in range(N_GROUPS):
            xg = xin.tile([P, TILES * D_FEAT], BF16, name="xg")
            if g == 0:
                nc.sync.dma_start(
                    out=xg[:].rearrange("p (j k) -> p j k", j=TILES), in_=X2.rearrange("(j p) k -> p j k", p=P)
                )
            else:
                nc.sync.dma_start(out=xg[:], in_=x_view[g - 1])
            words.append(xg[:].bitcast(F32).rearrange("p (j w) -> p j w", j=TILES))

        ident = const.tile([P, P], F32, name="ident")
        make_identity(nc, ident[:])

        banks, squares, sums, norms, operands, scaled, results = {}, {}, {}, {}, {}, {}, {}

        def transpose_unit(b):
            bank = psum_t.tile([P, 2 * UNIT], F32, name="bank")
            banks[b] = bank[:].bitcast(BF16)
            for u in range(2):
                for h in range(PAIR):
                    nc.tensor.transpose(
                        bank[:, (u * PAIR + h) * P : (u * PAIR + h + 1) * P],
                        words[b // 2][:, (b % 2) * PAIR + h, u * P : (u + 1) * P],
                        ident[:],
                    )

        transpose_unit(0)
        transpose_unit(1)

        absx = const.tile([P, VAR_COL + 1], F32, name="absx")
        expx = const.tile([P, VAR_COL + 1], F32, name="expx")
        logx = const.tile([P, VAR_COL + 1], F32, name="logx")
        soft = const.tile([P, VAR_COL + 1], F32, name="soft")
        invl = const.tile([P, PACK], F32, name="invl")
        sinv = const.tile([P, PACK], F32, name="sinv")
        lnv = const.tile([P, 1], F32, name="lnv")

        def softplus_log(cols, width):
            nc.vector.scalar_tensor_tensor(
                out=absx[:, cols], in0=raw[:, cols], scalar=-1.0, in1=raw[:, cols], op0=ALU.mult, op1=ALU.max
            )
            nc.gpsimd.tensor_tensor(out=expx[:, cols], in0=base[:, 0:width], in1=absx[:, cols], op=ALU.pow)
            nc.scalar.activation(out=logx[:, cols], in_=expx[:, cols], func=ACT.Ln, bias=one_col[:, 0:1])

        def softplus_sum(cols):
            nc.vector.scalar_tensor_tensor(
                out=soft[:, cols], in0=raw[:, cols], scalar=0.0, in1=logx[:, cols], op0=ALU.max, op1=ALU.add
            )

        softplus_log(slice(0, PACK), PACK)
        softplus_sum(slice(0, PACK))
        nc.vector.reciprocal(out=invl[:], in_=soft[:, 0:PACK])
        nc.vector.tensor_scalar(out=sinv[:], in0=invl[:], scalar1=SQRT_HALF, scalar2=None, op0=ALU.mult)
        invl_rep = invl[:].unsqueeze(1).to_broadcast([P, UNIT, PACK])
        var_col = slice(VAR_COL, VAR_COL + 1)

        x2_codes = const.tile([P, M_ROWS], U32, name="x2_codes", align_bytes=64)
        x2_scales = const.tile([P, M_ROWS], U8, name="x2_scales", align_bytes=64)
        col_term = const.tile([P, M_ROWS], F32, name="col_term")

        def scale_unit(b):
            if b % 2 == 0:
                grouped = pairs.tile([P, GROUP, PACK], BF16, name="grouped", align_bytes=64)
                scaled[b // 2] = grouped
            rows = slice((b % 2) * UNIT, (b % 2 + 1) * UNIT)
            nc.vector.tensor_tensor(
                out=scaled[b // 2][:, rows, :].rearrange("p r (u e) -> p r u e", e=2),
                in0=banks[b].rearrange("p (u r e) -> p r u e", u=2, e=2),
                in1=invl_rep.rearrange("p r (u e) -> p r u e", e=2),
                op=ALU.mult,
            )

        def square_unit(b):
            slots = banks[b].rearrange("p (u r e) -> p u e r", u=2, e=2)
            sq = work.tile([P, PACK, UNIT], F32, name="sq")
            squares[b] = sq
            for u in range(2):
                for e in range(2):
                    t = 2 * u + e
                    nc.scalar.activation(
                        out=sq[:, t, :], in_=slots[:, u, e, :], func=ACT.Square, scale=sinv[:, t : t + 1]
                    )

        def quantise_group(g):
            if g == 0:
                codes, scales = x2_codes[:], x2_scales[:]
            else:
                codes_t = held.tile([P, GROUP], U32, name="codes", align_bytes=64)
                scales_t = held.tile([P, GROUP], U8, name="scales", align_bytes=64)
                codes, scales = codes_t[:], scales_t[:]
            nc.vector.quantize_mx(
                out=codes.bitcast(FP8X4), scales=scales, in_=scaled[g][:].rearrange("p r t -> p (r t)")
            )
            for b in (2 * g, 2 * g + 1):
                rows = slice((b % 2) * UNIT, (b % 2 + 1) * UNIT)
                operands[b] = (codes[:, rows], scales[:, rows])

        def sum_unit(b):
            sums_t = psum_s.tile([P, TILES, P], F32, name="sums")
            sums[b] = sums_t
            for h in range(PAIR):
                for t in range(PACK):
                    nc.tensor.matmul(
                        out=sums[b][:, h, :],
                        lhsT=squares[b][:, t, h * P : (h + 1) * P],
                        rhs=ident[:],
                        is_transpose=True,
                        start=(t == 0),
                        stop=(t == PACK - 1),
                    )

        def reduce_unit(b):
            norm = small.tile([P, PAIR], F32, name="norm")
            norms[b] = norm
            if b in VECTOR_SUMS:
                nc.vector.tensor_reduce(out=norm[:], in_=sums[b][:, 0:PAIR, :], axis=AXIS.X, op=ALU.add)
            else:
                for h in reversed(range(PAIR)):
                    junk = work.tile([P, P], BF16, name="junk")
                    nc.scalar.activation(out=junk[:], in_=sums[b][:, h, :], func=ACT.Copy, accum_out=norm[:, h : h + 1])

        def spread_column_norms():
            yn_ps = psum_s.tile([P, TILES, P], F32, name="sums")
            for j in range(TILES):
                nc.tensor.matmul(
                    out=yn_ps[:, j, :],
                    lhsT=norms[j // PAIR][:, j % PAIR : j % PAIR + 1].to_broadcast([P, P]),
                    rhs=ident[:],
                    start=True,
                    stop=True,
                )
            return yn_ps

        def multiply_tile(b, h):
            codes, scales = operands[b]
            cols = slice(h * P, (h + 1) * P)
            cross = psum_c.tile([P, M_ROWS], F32, name="cross")
            nc.tensor.matmul_mx(
                out=cross[:],
                lhsT=codes[:, cols].bitcast(FP8X4),
                lhsT_scale=scales[:, cols],
                rhs=x2_codes[:].bitcast(FP8X4),
                rhs_scale=x2_scales[:],
                start=True,
                stop=True,
            )
            return cross

        def finish_tiles(g, first, count):
            flat = results[g][:, first : first + count, :].rearrange("p j m -> p (j m)")
            nc.scalar.activation(out=flat, in_=flat, func=ACT.Exp, bias=lnv[:, 0:1])
            nc.sync.dma_start(out=out_view[g - 1][:, first * M_ROWS : (first + count) * M_ROWS], in_=flat)

        def exponent_tile(b, h, cross):
            g, j = b // 2, (b % 2) * PAIR + h
            if g not in results:
                res = outp.tile([P, TILES, M_ROWS], F32, name="res")
                results[g] = res
            row = results[g][:, j, :]
            nc.vector.scalar_tensor_tensor(
                out=row, in0=cross[:], scalar=norms[b][:, h : h + 1], in1=col_term[:], op0=ALU.subtract, op1=ALU.add
            )
            if b == N_UNITS - 1:
                nc.vector.tensor_scalar(out=row, in0=row, scalar1=0.0, scalar2=None, op0=ALU.min)
                finish_tiles(g, j, 1)
            else:
                nc.gpsimd.tensor_scalar(out=row, in0=row, scalar1=0.0, scalar2=-1.0e30, op0=ALU.min, op1=ALU.max)

        yn_ps = None
        for s in range(N_UNITS + LAG_MULTIPLY):
            b = s - LAG_MULTIPLY
            live = b >= 2
            crosses = {}
            if live:
                for h in reversed(range(PAIR)):
                    crosses[h] = multiply_tile(b, h)
            if s + 2 < N_UNITS:
                transpose_unit(s + 2)
            if s == 1:
                softplus_log(var_col, 1)
            if s == 2:
                softplus_sum(var_col)
                nc.scalar.activation(out=lnv[:], in_=soft[:, var_col], func=ACT.Ln)
            if s == 3:
                yn_ps = spread_column_norms()
            if s + 1 < N_UNITS:
                square_unit(s + 1)
            if s < N_UNITS:
                scale_unit(s)
            if s == 0:
                square_unit(0)
            if s == 4:
                nc.vector.tensor_scalar(
                    out=col_term[:], in0=yn_ps[:].rearrange("p j r -> p (j r)"), scalar1=-1.0, scalar2=None, op0=ALU.mult
                )
            if s < N_UNITS:
                sum_unit(s)
            if 1 <= s <= N_UNITS:
                reduce_unit(s - 1)
            for done in range(2, N_UNITS - 1):
                if b - done == (LAG_EXP if done < N_UNITS - 2 else 1):
                    finish_tiles(done // 2, (done % 2) * PAIR, PAIR)
            if live:
                exponent_tile(b, 1, crosses[1])
            if s % 2 == 0 and 2 <= s <= N_UNITS:
                quantise_group(s // 2 - 1)
            if live:
                exponent_tile(b, 0, crosses[0])
